import numpy as np
import ml_dtypes


def mxq(x, axis, fmt="e4m3"):
    dtype, down = {"e4m3": (ml_dtypes.float8_e4m3fn, 7), "e5m2": (ml_dtypes.float8_e5m2, 14)}[fmt]
    v = np.moveaxis(np.asarray(x, np.float32).astype(ml_dtypes.bfloat16).astype(np.float64), axis, -1)
    blocks = v.reshape(v.shape[:-1] + (-1, 32))
    amax = np.abs(blocks).max(-1, keepdims=True)
    byte = np.maximum(np.where(amax > 0, np.frexp(amax)[1] - 1 + 127, 0) - down, 1)
    scale = np.exp2(byte - 127.0)
    codes = (blocks / scale).astype(np.float32).astype(dtype).astype(np.float64)
    return np.moveaxis((codes * scale).reshape(v.shape), -1, axis)


WIDE = False


def mx_kscale(k):
    if not WIDE:
        return np.ones(k)
    levels = np.array([10, -10, 5, -5, 0])
    if k % 512:
        return np.exp2(np.random.permutation(np.resize(levels, k // 32))).repeat(32)
    a = np.empty((k // 512, 16))
    for p in range(k // 512):
        a[p, :8] = np.random.permutation(np.resize(levels, 8))
        for g in range(8):
            far = levels[np.abs(levels - a[p, g]) >= 10]
            a[p, g + 8] = far[np.random.randint(len(far))]
    return np.exp2(a.ravel()).repeat(32)


BF16 = ml_dtypes.bfloat16


def bf(x):
    return np.asarray(x, np.float32).astype(BF16)


def f64(x):
    return np.asarray(x).astype(np.float64)


B, IN, HID, BLK, OUT = 4096, 512, 1024, 512, 10
NB = HID // BLK


def setup_inputs():
    s = mx_kscale(IN)
    t = np.tile(mx_kscale(BLK), NB)
    return {
        "x": bf(np.random.standard_normal((B, IN)) * s),
        "W1": bf(np.random.standard_normal((HID, IN)) / np.sqrt(IN) / s * t[:, None]),
        "b1": bf(np.random.standard_normal(HID) * 0.3 * t),
        "Wb": bf(np.random.standard_normal((NB, BLK, BLK)) * 1.4 / np.sqrt(BLK) / t.reshape(NB, 1, BLK)),
        "bb": bf(np.random.standard_normal(HID) * 0.3),
    }


def reference(x, W1, b1, Wb, bb):
    h = np.maximum((mxq(f64(x), 1, "e4m3") @ mxq(f64(W1), 1, "e4m3").T) + f64(b1), 0.0)
    hb = h.reshape(B, NB, BLK)
    yb = (mxq(hb, 2, "e4m3").transpose(1, 0, 2) @ mxq(f64(Wb), 2, "e4m3").transpose(0, 2, 1)).transpose(1, 0, 2)
    return np.maximum(yb.reshape(B, HID) + f64(bb), 0.0)

@@ -1,0 +1,270 @@
+from contextlib import ExitStack
+
+import concourse.bass as bass
+import concourse.mybir as mybir
+import concourse.tile as tile
+from concourse.masks import make_identity
+
+F32 = mybir.dt.float32
+BF16 = mybir.dt.bfloat16
+U32 = mybir.dt.uint32
+U8 = mybir.dt.uint8
+FP8X4 = mybir.dt.float8_e4m3fn_x4
+ALU = mybir.AluOpType
+ACT = mybir.ActivationFunctionType
+
+P = 128
+B, IN, HID, BLK = 4096, 512, 1024, 512
+NB = HID // BLK
+ROWS_PER_PART = B // P
+TILES = 4
+CHUNKS = ROWS_PER_PART // TILES
+CW = TILES * P
+
+FLOPS = 2 * B * HID * IN + 2 * B * HID * BLK
+
+
+def relu2_engines(c):
+    return ("S", "V", "S", "V") if c == CHUNKS - 1 else (("S", "S", "S", "S") if c >= 4 else ("S", "S", "S", "V"))
+
+PINNED = False
+
+
+def tile_blockdiagmnistconvertible_pa_t_kernel(tc, x, W1, b1, Wb, bb, out):
+    nc = tc.nc
+    with ExitStack() as ctx:
+        const = ctx.enter_context(tc.tile_pool(name="const", bufs=1))
+        xin = ctx.enter_context(tc.tile_pool(name="xin", bufs=1))
+        win = ctx.enter_context(tc.tile_pool(name="win", bufs=1))
+        wq = ctx.enter_context(tc.tile_pool(name="wq", bufs=1))
+        wgp = ctx.enter_context(tc.tile_pool(name="wgp", bufs=2))
+        xq = ctx.enter_context(tc.tile_pool(name="xq", bufs=4))
+        hp = ctx.enter_context(tc.tile_pool(name="hp", bufs=4))
+        zp = ctx.enter_context(tc.tile_pool(name="zp", bufs=4))
+        ps_tr = ctx.enter_context(tc.psum_pool(name="ps_tr", bufs=2))
+        ps_s1 = ctx.enter_context(tc.psum_pool(name="ps_s1", bufs=3))
+        ps_s2 = ctx.enter_context(tc.psum_pool(name="ps_s2", bufs=3))
+        if PINNED:
+            ctx.enter_context(tc.manual_schedule())
+
+        x_v = x.rearrange("(p i) k -> p (i k)", i=ROWS_PER_PART)
+        out_v = out.rearrange("(p i) o -> p (i o)", i=ROWS_PER_PART)
+
+        xs = []
+        for c in range(CHUNKS):
+            xs.append(xin.tile([P, TILES * IN], BF16, name="xs%d" % c))
+        w1s = [win.tile([P, 4 * IN], BF16, name="w1s%d" % n) for n in range(NB)]
+        wbs = [win.tile([P, 4 * BLK], BF16, name="wbs%d" % n) for n in range(NB)]
+
+        def load_x(c):
+            nc.sync.dma_start(out=xs[c][:], in_=x_v[:, c * TILES * IN : (c + 1) * TILES * IN])
+
+        def load_w1(n):
+            nc.sync.dma_start(
+                out=w1s[n][:],
+                in_=W1[n * BLK : (n + 1) * BLK, :].rearrange("(p t) k -> p (t k)", t=4),
+            )
+
+        def load_wb(n):
+            nc.sync.dma_start(
+                out=wbs[n][:].rearrange("p (j k) -> p j k", j=4),
+                in_=Wb[n].rearrange("(j p) k -> p j k", p=P),
+            )
+
+        b1b = const.tile([P, 2 * 4], BF16, name="b1b")
+        bbrow = const.tile([P, HID], BF16, name="bbrow")
+        ones = const.tile([P, P], BF16, name="ones")
+        bbb = const.tile([P, HID], F32, name="bbb")
+        nc.scalar.dma_start(
+            out=b1b[:].rearrange("p (n t) -> p n t", t=4),
+            in_=b1.rearrange("(n p t) -> p n t", n=NB, t=4),
+        )
+        load_x(0)
+        load_w1(0)
+        load_w1(1)
+        load_x(1)
+        load_wb(0)
+        load_wb(1)
+        for c in range(2, CHUNKS):
+            load_x(c)
+
+        ident = const.tile([P, P], F32, name="ident")
+        make_identity(nc, ident[:])
+        nc.gpsimd.memset(bbrow[:], 0.0)
+        nc.gpsimd.memset(ones[:], 1.0)
+        nc.scalar.dma_start(out=bbrow[0:1, :], in_=bb.rearrange("(o n) -> o n", o=1))
+
+        def spread_bb():
+            for n in range(NB):
+                pb = ps_tr.tile([P, 512], F32, name="pt")
+                nc.tensor.matmul(
+                    out=pb[:],
+                    lhsT=ones[:],
+                    rhs=bbrow[:, n * BLK : (n + 1) * BLK],
+                    start=True,
+                    stop=True,
+                )
+                nc.scalar.copy(out=bbb[:, n * BLK : (n + 1) * BLK], in_=pb[:])
+        b1f = const.tile([P, 2 * 4], F32, name="b1f")
+        nc.vector.tensor_copy(out=b1f[:], in_=b1b[:])
+
+        def copy_words(eng, dst, src):
+            if eng == "S":
+                nc.scalar.copy(out=dst, in_=src)
+            else:
+                nc.vector.tensor_copy(out=dst, in_=src)
+
+        def transpose_group(src_words, grouped, engines):
+            g32 = grouped[:].bitcast(F32).rearrange("p (c u) -> p c u", u=2)
+            for h in range(2):
+                pt = ps_tr.tile([P, 512], F32, name="pt")
+                for il in range(2):
+                    for u in range(2):
+                        nc.tensor.transpose(
+                            pt[:, u * 256 + il * P : u * 256 + (il + 1) * P],
+                            src_words(2 * h + il, u),
+                            ident[:],
+                        )
+                copy_words(
+                    engines[h],
+                    g32[:, h * 256 : (h + 1) * 256, :],
+                    pt[:].rearrange("p (u c) -> p c u", u=2),
+                )
+
+        def quantise(grouped, codes, scales):
+            nc.vector.quantize_mx(out=codes[:].bitcast(FP8X4), scales=scales[:], in_=grouped[:])
+
+        w1c = [wq.tile([P, 512], U32, name="w1c%d" % n, align_bytes=64) for n in range(NB)]
+        w1sc = [wq.tile([P, 512], U8, name="w1sc%d" % n, align_bytes=64) for n in range(NB)]
+        wbc = [wq.tile([P, 512], U32, name="wbc%d" % n, align_bytes=64) for n in range(NB)]
+        wbsc = [wq.tile([P, 512], U8, name="wbsc%d" % n, align_bytes=64) for n in range(NB)]
+
+        def prep_w1(n):
+            w32 = w1s[n][:].bitcast(F32).rearrange("p (t q u) -> p t q u", t=4, u=2)
+            wg = wgp.tile([P, 2048], BF16, name="wg", align_bytes=64)
+            transpose_group(lambda t, u: w32[:, t, :, u], wg, ("V", "S"))
+            quantise(wg, w1c[n], w1sc[n])
+
+        def prep_wb(n):
+            w32 = wbs[n][:].bitcast(F32).rearrange("p (j q u) -> p j q u", j=4, u=2)
+            wg = wgp.tile([P, 2048], BF16, name="wg", align_bytes=64)
+            transpose_group(lambda j, u: w32[:, j, :, u], wg, ("V", "S"))
+            quantise(wg, wbc[n], wbsc[n])
+
+        xcs = {}
+
+        def xpath(c):
+            x32 = xs[c][:].bitcast(F32).rearrange("p (i q u) -> p i q u", i=TILES, u=2)
+            xg = xq.tile([P, 2048], BF16, name="xg", align_bytes=64)
+            transpose_group(lambda i, u: x32[:, i, :, u], xg, ("S", "S"))
+            xc = xq.tile([P, CW], U32, name="xc", align_bytes=64)
+            xsc = xq.tile([P, CW], U8, name="xsc", align_bytes=64)
+            quantise(xg, xc, xsc)
+            xcs[c] = (xc, xsc)
+
+        hcs = {}
+        hTs = {}
+        hgs = {}
+
+        def stage1(c):
+            xc, xsc = xcs[c]
+            for n in range(NB):
+                hT = hp.tile([P, 4 * CW], BF16, name="hT")
+                for t in range(4):
+                    acc = ps_s1.tile([P, CW], F32, name="acc1")
+                    nc.tensor.matmul_mx(
+                        out=acc[:],
+                        lhsT=w1c[n][:, t * P : (t + 1) * P].bitcast(FP8X4),
+                        lhsT_scale=w1sc[n][:, t * P : (t + 1) * P],
+                        rhs=xc[:].bitcast(FP8X4),
+                        rhs_scale=xsc[:],
+                        start=True,
+                        stop=True,
+                    )
+                    nc.scalar.activation(
+                        out=hT[:, t * CW : (t + 1) * CW],
+                        in_=acc[:],
+                        func=ACT.Relu,
+                        bias=b1f[:, 4 * n + t : 4 * n + t + 1],
+                        scale=1.0,
+                    )
+                hTs[(c, n)] = hT
+
+        def regroup(c, n):
+            hg = hp.tile([P, 4 * CW], BF16, name="hg", align_bytes=64)
+            nc.vector.tensor_copy(
+                out=hg[:].rearrange("p (c i t) -> p c t i", i=4, t=4),
+                in_=hTs[(c, n)][:].rearrange("p (t c i) -> p c t i", t=4, i=4),
+            )
+            hgs[(c, n)] = hg
+
+        def h_quantise(c, n):
+            hc = hp.tile([P, CW], U32, name="hc%d" % n, align_bytes=64)
+            hsc = hp.tile([P, CW], U8, name="hsc%d" % n, align_bytes=64)
+            quantise(hgs[(c, n)], hc, hsc)
+            hcs[(c, n)] = (hc, hsc)
+
+        def next_h_step(c, step):
+            if step < 2:
+                regroup(c, step)
+            else:
+                h_quantise(c, step - 2)
+
+        def relu2(eng, ap):
+            if eng == "V":
+                nc.vector.tensor_scalar_max(out=ap, in0=ap, scalar1=0.0)
+            elif eng == "S":
+                nc.scalar.activation(out=ap, in_=ap, func=ACT.Relu)
+            else:
+                nc.gpsimd.tensor_scalar(
+                    out=ap, in0=ap, scalar1=0.0, scalar2=0.0, op0=ALU.max, op1=ALU.add
+                )
+
+        def stage2(c):
+            z = zp.tile([P, TILES * HID], F32, name="z")
+            for il in range(TILES):
+                for n in range(NB):
+                    hc, hsc = hcs[(c, n)]
+                    acc = ps_s2.tile([P, BLK], F32, name="acc2")
+                    nc.tensor.matmul_mx(
+                        out=acc[:],
+                        lhsT=hc[:, il * P : (il + 1) * P].bitcast(FP8X4),
+                        lhsT_scale=hsc[:, il * P : (il + 1) * P],
+                        rhs=wbc[n][:].bitcast(FP8X4),
+                        rhs_scale=wbsc[n][:],
+                        start=True,
+                        stop=True,
+                    )
+                    nc.vector.tensor_tensor(
+                        out=z[:, il * HID + n * BLK : il * HID + (n + 1) * BLK],
+                        in0=acc[:],
+                        in1=bbb[:, n * BLK : (n + 1) * BLK],
+                        op=ALU.add,
+                    )
+                relu2(relu2_engines(c)[il], z[:, il * HID : (il + 1) * HID])
+                if c + 1 < CHUNKS:
+                    next_h_step(c + 1, il)
+                rows = 1 if c == CHUNKS - 1 else 2
+                if (il + 1) % rows == 0:
+                    lo = (il + 1 - rows) * HID
+                    hi = (il + 1) * HID
+                    nc.sync.dma_start(
+                        out=out_v[:, c * TILES * HID + lo : c * TILES * HID + hi], in_=z[:, lo:hi]
+                    )
+
+        xpath(0)
+        prep_w1(0)
+        prep_w1(1)
+        xpath(1)
+        stage1(0)
+        spread_bb()
+        prep_wb(0)
+        prep_wb(1)
+        for step in range(4):
+            next_h_step(0, step)
+        for c in range(1, CHUNKS):
+            if c + 1 < CHUNKS:
+                xpath(c + 1)
+            stage1(c)
+            stage2(c - 1)
+        stage2(CHUNKS - 1)

@@ -21,11 +21,13 @@ TILES = 4
 CHUNKS = ROWS_PER_PART // TILES
 CW = TILES * P
 
+F32_MAX = 3.4028234663852886e38
+
 FLOPS = 2 * B * HID * IN + 2 * B * HID * BLK
 
 
 def relu2_engines(c):
-    return ("S", "V", "S", "V") if c == CHUNKS - 1 else (("S", "S", "S", "S") if c >= 4 else ("S", "S", "S", "V"))
+    return ("S", "V", "S", "V") if c == CHUNKS - 1 else ("G", "S", "G", "S")
 
 PINNED = False
 
@@ -217,7 +219,7 @@ def tile_blockdiagmnistconvertible_pa_t_kernel(tc, x, W1, b1, Wb, bb, out):
                 nc.scalar.activation(out=ap, in_=ap, func=ACT.Relu)
             else:
                 nc.gpsimd.tensor_scalar(
-                    out=ap, in0=ap, scalar1=0.0, scalar2=0.0, op0=ALU.max, op1=ALU.add
+                    out=ap, in0=ap, scalar1=F32_MAX, scalar2=0.0, op0=ALU.min, op1=ALU.max
                 )
 
         def stage2(c):

@@ -20,16 +20,9 @@ ROWS_PER_PART = B // P
 TILES = 4
 CHUNKS = ROWS_PER_PART // TILES
 CW = TILES * P
-
 F32_MAX = 3.4028234663852886e38
 
 FLOPS = 2 * B * HID * IN + 2 * B * HID * BLK
-
-
-def relu2_engines(c):
-    return ("S", "V", "S", "V") if c == CHUNKS - 1 else ("G", "S", "G", "S")
-
-PINNED = False
 
 
 def tile_blockdiagmnistconvertible_pa_t_kernel(tc, x, W1, b1, Wb, bb, out):
@@ -42,12 +35,11 @@ def tile_blockdiagmnistconvertible_pa_t_kernel(tc, x, W1, b1, Wb, bb, out):
         wgp = ctx.enter_context(tc.tile_pool(name="wgp", bufs=2))
         xq = ctx.enter_context(tc.tile_pool(name="xq", bufs=4))
         hp = ctx.enter_context(tc.tile_pool(name="hp", bufs=4))
-        zp = ctx.enter_context(tc.tile_pool(name="zp", bufs=4))
+        zp = ctx.enter_context(tc.tile_pool(name="zp", bufs=6))
         ps_tr = ctx.enter_context(tc.psum_pool(name="ps_tr", bufs=2))
         ps_s1 = ctx.enter_context(tc.psum_pool(name="ps_s1", bufs=3))
         ps_s2 = ctx.enter_context(tc.psum_pool(name="ps_s2", bufs=3))
-        if PINNED:
-            ctx.enter_context(tc.manual_schedule())
+        ctx.enter_context(tc.manual_schedule())
 
         x_v = x.rearrange("(p i) k -> p (i k)", i=ROWS_PER_PART)
         out_v = out.rearrange("(p i) o -> p (i o)", i=ROWS_PER_PART)
@@ -74,41 +66,35 @@ def tile_blockdiagmnistconvertible_pa_t_kernel(tc, x, W1, b1, Wb, bb, out):
             )
 
         b1b = const.tile([P, 2 * 4], BF16, name="b1b")
+        b1f = const.tile([P, 2 * 4], F32, name="b1f")
         bbrow = const.tile([P, HID], BF16, name="bbrow")
         ones = const.tile([P, P], BF16, name="ones")
         bbb = const.tile([P, HID], F32, name="bbb")
+        ident = const.tile([P, P], F32, name="ident")
         nc.scalar.dma_start(
             out=b1b[:].rearrange("p (n t) -> p n t", t=4),
             in_=b1.rearrange("(n p t) -> p n t", n=NB, t=4),
         )
+        make_identity(nc, ident[:])
+        nc.gpsimd.memset(bbrow[:], 0.0)
+        nc.gpsimd.memset(ones[:], 1.0)
         load_x(0)
         load_w1(0)
         load_w1(1)
         load_x(1)
+        nc.sync.dma_start(out=bbrow[0:1, :], in_=bb.rearrange("(o n) -> o n", o=1))
         load_wb(0)
         load_wb(1)
         for c in range(2, CHUNKS):
             load_x(c)
-
-        ident = const.tile([P, P], F32, name="ident")
-        make_identity(nc, ident[:])
-        nc.gpsimd.memset(bbrow[:], 0.0)
-        nc.gpsimd.memset(ones[:], 1.0)
-        nc.scalar.dma_start(out=bbrow[0:1, :], in_=bb.rearrange("(o n) -> o n", o=1))
-
-        def spread_bb():
-            for n in range(NB):
-                pb = ps_tr.tile([P, 512], F32, name="pt")
-                nc.tensor.matmul(
-                    out=pb[:],
-                    lhsT=ones[:],
-                    rhs=bbrow[:, n * BLK : (n + 1) * BLK],
-                    start=True,
-                    stop=True,
-                )
-                nc.scalar.copy(out=bbb[:, n * BLK : (n + 1) * BLK], in_=pb[:])
-        b1f = const.tile([P, 2 * 4], F32, name="b1f")
         nc.vector.tensor_copy(out=b1f[:], in_=b1b[:])
+
+        def spread_bb(n, eng):
+            pb = ps_tr.tile([P, 512], F32, name="pt")
+            nc.tensor.matmul(
+                out=pb[:], lhsT=ones[:], rhs=bbrow[:, n * BLK : (n + 1) * BLK], start=True, stop=True
+            )
+            copy_words(eng, bbb[:, n * BLK : (n + 1) * BLK], pb[:])
 
         def copy_words(eng, dst, src):
             if eng == "S":
@@ -116,22 +102,21 @@ def tile_blockdiagmnistconvertible_pa_t_kernel(tc, x, W1, b1, Wb, bb, out):
             else:
                 nc.vector.tensor_copy(out=dst, in_=src)
 
-        def transpose_group(src_words, grouped, engines):
+        def transpose_half(src_words, grouped, h, eng):
             g32 = grouped[:].bitcast(F32).rearrange("p (c u) -> p c u", u=2)
-            for h in range(2):
-                pt = ps_tr.tile([P, 512], F32, name="pt")
-                for il in range(2):
-                    for u in range(2):
-                        nc.tensor.transpose(
-                            pt[:, u * 256 + il * P : u * 256 + (il + 1) * P],
-                            src_words(2 * h + il, u),
-                            ident[:],
-                        )
-                copy_words(
-                    engines[h],
-                    g32[:, h * 256 : (h + 1) * 256, :],
-                    pt[:].rearrange("p (u c) -> p c u", u=2),
-                )
+            pt = ps_tr.tile([P, 512], F32, name="pt")
+            for il in range(2):
+                for u in range(2):
+                    nc.tensor.transpose(
+                        pt[:, u * 256 + il * P : u * 256 + (il + 1) * P],
+                        src_words(2 * h + il, u),
+                        ident[:],
+                    )
+            copy_words(
+                eng,
+                g32[:, h * 256 : (h + 1) * 256, :],
+                pt[:].rearrange("p (u c) -> p c u", u=2),
+            )
 
         def quantise(grouped, codes, scales):
             nc.vector.quantize_mx(out=codes[:].bitcast(FP8X4), scales=scales[:], in_=grouped[:])
@@ -140,59 +125,64 @@ def tile_blockdiagmnistconvertible_pa_t_kernel(tc, x, W1, b1, Wb, bb, out):
         w1sc = [wq.tile([P, 512], U8, name="w1sc%d" % n, align_bytes=64) for n in range(NB)]
         wbc = [wq.tile([P, 512], U32, name="wbc%d" % n, align_bytes=64) for n in range(NB)]
         wbsc = [wq.tile([P, 512], U8, name="wbsc%d" % n, align_bytes=64) for n in range(NB)]
+        w1g = [wq.tile([P, 2048], BF16, name="w1g%d" % n, align_bytes=64) for n in range(NB)]
+        wbg = [wq.tile([P, 2048], BF16, name="wbg%d" % n, align_bytes=64) for n in range(NB)]
+        xgs, xcs, hTs, hgs, hcs, zs = {}, {}, {}, {}, {}, {}
 
-        def prep_w1(n):
+        def w1_half(n, h, eng):
             w32 = w1s[n][:].bitcast(F32).rearrange("p (t q u) -> p t q u", t=4, u=2)
-            wg = wgp.tile([P, 2048], BF16, name="wg", align_bytes=64)
-            transpose_group(lambda t, u: w32[:, t, :, u], wg, ("V", "S"))
-            quantise(wg, w1c[n], w1sc[n])
+            transpose_half(lambda t, u: w32[:, t, :, u], w1g[n], h, eng)
 
-        def prep_wb(n):
+        def wb_half(n, h, eng):
             w32 = wbs[n][:].bitcast(F32).rearrange("p (j q u) -> p j q u", j=4, u=2)
-            wg = wgp.tile([P, 2048], BF16, name="wg", align_bytes=64)
-            transpose_group(lambda j, u: w32[:, j, :, u], wg, ("V", "S"))
-            quantise(wg, wbc[n], wbsc[n])
+            transpose_half(lambda j, u: w32[:, j, :, u], wbg[n], h, eng)
 
-        xcs = {}
-
-        def xpath(c):
+        def x_half(c, h, eng="S"):
+            if c >= CHUNKS:
+                return
+            if h == 0:
+                xg = xq.tile([P, 2048], BF16, name="xg", align_bytes=64)
+                xgs[c] = xg
             x32 = xs[c][:].bitcast(F32).rearrange("p (i q u) -> p i q u", i=TILES, u=2)
-            xg = xq.tile([P, 2048], BF16, name="xg", align_bytes=64)
-            transpose_group(lambda i, u: x32[:, i, :, u], xg, ("S", "S"))
+            transpose_half(lambda i, u: x32[:, i, :, u], xgs[c], h, eng)
+
+        def x_quant(c):
+            if c >= CHUNKS:
+                return
             xc = xq.tile([P, CW], U32, name="xc", align_bytes=64)
             xsc = xq.tile([P, CW], U8, name="xsc", align_bytes=64)
-            quantise(xg, xc, xsc)
+            quantise(xgs[c], xc, xsc)
             xcs[c] = (xc, xsc)
 
-        hcs = {}
-        hTs = {}
-        hgs = {}
-
-        def stage1(c):
-            xc, xsc = xcs[c]
-            for n in range(NB):
+        def s1(c, n, t, eng="S"):
+            if c >= CHUNKS:
+                return
+            if t == 0:
                 hT = hp.tile([P, 4 * CW], BF16, name="hT")
-                for t in range(4):
-                    acc = ps_s1.tile([P, CW], F32, name="acc1")
-                    nc.tensor.matmul_mx(
-                        out=acc[:],
-                        lhsT=w1c[n][:, t * P : (t + 1) * P].bitcast(FP8X4),
-                        lhsT_scale=w1sc[n][:, t * P : (t + 1) * P],
-                        rhs=xc[:].bitcast(FP8X4),
-                        rhs_scale=xsc[:],
-                        start=True,
-                        stop=True,
-                    )
-                    nc.scalar.activation(
-                        out=hT[:, t * CW : (t + 1) * CW],
-                        in_=acc[:],
-                        func=ACT.Relu,
-                        bias=b1f[:, 4 * n + t : 4 * n + t + 1],
-                        scale=1.0,
-                    )
                 hTs[(c, n)] = hT
+            xc, xsc = xcs[c]
+            acc = ps_s1.tile([P, CW], F32, name="acc1")
+            nc.tensor.matmul_mx(
+                out=acc[:],
+                lhsT=w1c[n][:, t * P : (t + 1) * P].bitcast(FP8X4),
+                lhsT_scale=w1sc[n][:, t * P : (t + 1) * P],
+                rhs=xc[:].bitcast(FP8X4),
+                rhs_scale=xsc[:],
+                start=True,
+                stop=True,
+            )
+            dst = hTs[(c, n)][:, t * CW : (t + 1) * CW]
+            bias = b1f[:, 4 * n + t : 4 * n + t + 1]
+            if eng == "S":
+                nc.scalar.activation(out=dst, in_=acc[:], func=ACT.Relu, bias=bias, scale=1.0)
+            else:
+                nc.vector.tensor_scalar(
+                    out=dst, in0=acc[:], scalar1=bias, scalar2=0.0, op0=ALU.add, op1=ALU.max
+                )
 
         def regroup(c, n):
+            if c >= CHUNKS:
+                return
             hg = hp.tile([P, 4 * CW], BF16, name="hg", align_bytes=64)
             nc.vector.tensor_copy(
                 out=hg[:].rearrange("p (c i t) -> p c t i", i=4, t=4),
@@ -200,17 +190,13 @@ def tile_blockdiagmnistconvertible_pa_t_kernel(tc, x, W1, b1, Wb, bb, out):
             )
             hgs[(c, n)] = hg
 
-        def h_quantise(c, n):
+        def h_quant(c, n):
+            if c >= CHUNKS:
+                return
             hc = hp.tile([P, CW], U32, name="hc%d" % n, align_bytes=64)
             hsc = hp.tile([P, CW], U8, name="hsc%d" % n, align_bytes=64)
             quantise(hgs[(c, n)], hc, hsc)
             hcs[(c, n)] = (hc, hsc)
-
-        def next_h_step(c, step):
-            if step < 2:
-                regroup(c, step)
-            else:
-                h_quantise(c, step - 2)
 
         def relu2(eng, ap):
             if eng == "V":
@@ -222,51 +208,124 @@ def tile_blockdiagmnistconvertible_pa_t_kernel(tc, x, W1, b1, Wb, bb, out):
                     out=ap, in0=ap, scalar1=F32_MAX, scalar2=0.0, op0=ALU.min, op1=ALU.max
                 )
 
-        def stage2(c):
-            z = zp.tile([P, TILES * HID], F32, name="z")
-            for il in range(TILES):
-                for n in range(NB):
-                    hc, hsc = hcs[(c, n)]
-                    acc = ps_s2.tile([P, BLK], F32, name="acc2")
-                    nc.tensor.matmul_mx(
-                        out=acc[:],
-                        lhsT=hc[:, il * P : (il + 1) * P].bitcast(FP8X4),
-                        lhsT_scale=hsc[:, il * P : (il + 1) * P],
-                        rhs=wbc[n][:].bitcast(FP8X4),
-                        rhs_scale=wbsc[n][:],
-                        start=True,
-                        stop=True,
-                    )
-                    nc.vector.tensor_tensor(
-                        out=z[:, il * HID + n * BLK : il * HID + (n + 1) * BLK],
-                        in0=acc[:],
-                        in1=bbb[:, n * BLK : (n + 1) * BLK],
-                        op=ALU.add,
-                    )
-                relu2(relu2_engines(c)[il], z[:, il * HID : (il + 1) * HID])
-                if c + 1 < CHUNKS:
-                    next_h_step(c + 1, il)
-                rows = 1 if c == CHUNKS - 1 else 2
-                if (il + 1) % rows == 0:
-                    lo = (il + 1 - rows) * HID
-                    hi = (il + 1) * HID
-                    nc.sync.dma_start(
-                        out=out_v[:, c * TILES * HID + lo : c * TILES * HID + hi], in_=z[:, lo:hi]
-                    )
+        ADDS = ((1, 0), (1, 1), (0, 1), (0, 0))
 
-        xpath(0)
-        prep_w1(0)
-        prep_w1(1)
-        xpath(1)
-        stage1(0)
-        spread_bb()
-        prep_wb(0)
-        prep_wb(1)
-        for step in range(4):
-            next_h_step(0, step)
-        for c in range(1, CHUNKS):
-            if c + 1 < CHUNKS:
-                xpath(c + 1)
-            stage1(c)
-            stage2(c - 1)
-        stage2(CHUNKS - 1)
+        def s2(c, r, j):
+            if c < 0:
+                return
+            row, n = ADDS[j]
+            if j == 0:
+                z = zp.tile([P, 2 * HID], F32, name="z")
+                zs[(c, r)] = z
+            z = zs[(c, r)]
+            il = 2 * r + row
+            hc, hsc = hcs[(c, n)]
+            acc = ps_s2.tile([P, BLK], F32, name="acc2")
+            nc.tensor.matmul_mx(
+                out=acc[:],
+                lhsT=hc[:, il * P : (il + 1) * P].bitcast(FP8X4),
+                lhsT_scale=hsc[:, il * P : (il + 1) * P],
+                rhs=wbc[n][:].bitcast(FP8X4),
+                rhs_scale=wbsc[n][:],
+                start=True,
+                stop=True,
+            )
+            nc.vector.tensor_tensor(
+                out=z[:, row * HID + n * BLK : row * HID + (n + 1) * BLK],
+                in0=acc[:],
+                in1=bbb[:, n * BLK : (n + 1) * BLK],
+                op=ALU.add,
+            )
+
+        def relu_row(c, r, row, eng):
+            if c < 0:
+                return
+            z = zs[(c, r)]
+            relu2(eng, z[:, row * HID : (row + 1) * HID])
+
+        def store(c, r):
+            if c < 0:
+                return
+            base = c * TILES * HID + r * 2 * HID
+            nc.sync.dma_start(out=out_v[:, base : base + 2 * HID], in_=zs[(c, r)][:])
+
+        def store_row(c, r, row):
+            base = c * TILES * HID + r * 2 * HID + row * HID
+            z = zs[(c, r)]
+            nc.sync.dma_start(
+                out=out_v[:, base : base + HID], in_=z[:, row * HID : (row + 1) * HID]
+            )
+
+        x_half(0, 0, "S")
+        x_half(0, 1, "V")
+        w1_half(0, 0, "S")
+        x_quant(0)
+        w1_half(0, 1, "V")
+        w1_half(1, 0, "S")
+        quantise(w1g[0], w1c[0], w1sc[0])
+        w1_half(1, 1, "V")
+        for t in range(4):
+            s1(0, 0, t, "SV"[t % 2])
+            if t == 0:
+                quantise(w1g[1], w1c[1], w1sc[1])
+        x_half(1, 0, "S")
+        wb_half(0, 0, "V")
+        for t in range(4):
+            s1(0, 1, t, "SV"[t % 2])
+            if t == 0:
+                regroup(0, 0)
+        x_half(1, 1, "S")
+        wb_half(0, 1, "V")
+        x_quant(1)
+        wb_half(1, 0, "S")
+        regroup(0, 1)
+        quantise(wbg[0], wbc[0], wbsc[0])
+        h_quant(0, 0)
+        wb_half(1, 1, "S")
+        spread_bb(0, "S")
+        spread_bb(1, "S")
+        quantise(wbg[1], wbc[1], wbsc[1])
+        h_quant(0, 1)
+        x_half(2, 0)
+        x_half(2, 1)
+        s1(1, 0, 0)
+        s1(1, 0, 1)
+        x_quant(2)
+
+        for c in range(CHUNKS):
+            last = c == CHUNKS - 1
+            s2(c - 1, 1, 3)
+            s1(c + 1, 0, 2)
+            relu_row(c - 1, 1, 0, "G")
+            if c > 0:
+                store(c - 1, 1)
+            s2(c, 0, 0)
+            s1(c + 1, 0, 3)
+            s2(c, 0, 1)
+            s1(c + 1, 1, 0)
+            s2(c, 0, 2)
+            s1(c + 1, 1, 1)
+            relu_row(c, 0, 1, "S")
+            regroup(c + 1, 0)
+            s1(c + 1, 1, 2)
+            s2(c, 0, 3)
+            relu_row(c, 0, 0, "G")
+            store(c, 0)
+            s1(c + 1, 1, 3)
+            s2(c, 1, 0)
+            s2(c, 1, 1)
+            s2(c, 1, 2)
+            x_half(c + 3, 0)
+            x_half(c + 3, 1)
+            relu_row(c, 1, 1, "S")
+            if last:
+                store_row(c, 1, 1)
+            regroup(c + 1, 1)
+            h_quant(c + 1, 0)
+            x_quant(c + 3)
+            h_quant(c + 1, 1)
+            s1(c + 2, 0, 0)
+            s1(c + 2, 0, 1)
+        s2(CHUNKS - 1, 1, 3)
+        relu_row(CHUNKS - 1, 1, 0, "V")
+        store_row(CHUNKS - 1, 1, 0)

@@ -81,16 +81,14 @@ def tile_blockdiagmnistconvertible_pa_t_kernel(tc, x, W1, b1, Wb, bb, out):
         load_x(0)
         load_w1(0)
         load_w1(1)
-        load_x(1)
         nc.sync.dma_start(out=bbrow[0:1, :], in_=bb.rearrange("(o n) -> o n", o=1))
+        load_x(1)
         load_wb(0)
         load_wb(1)
         for c in range(2, CHUNKS):
             load_x(c)
-        nc.vector.tensor_copy(out=b1f[:], in_=b1b[:])
-
         def spread_bb(n, eng):
-            pb = ps_tr.tile([P, 512], F32, name="pt")
+            pb = ps_s1.tile([P, CW], F32, name="acc1")
             nc.tensor.matmul(
                 out=pb[:], lhsT=ones[:], rhs=bbrow[:, n * BLK : (n + 1) * BLK], start=True, stop=True
             )
@@ -102,9 +100,12 @@ def tile_blockdiagmnistconvertible_pa_t_kernel(tc, x, W1, b1, Wb, bb, out):
             else:
                 nc.vector.tensor_copy(out=dst, in_=src)
 
-        def transpose_half(src_words, grouped, h, eng):
+        def transpose_half(src_words, grouped, h, eng, bank="T"):
             g32 = grouped[:].bitcast(F32).rearrange("p (c u) -> p c u", u=2)
-            pt = ps_tr.tile([P, 512], F32, name="pt")
+            if bank == "T":
+                pt = ps_tr.tile([P, 512], F32, name="pt")
+            else:
+                pt = ps_s2.tile([P, BLK], F32, name="acc2")
             for il in range(2):
                 for u in range(2):
                     nc.tensor.transpose(
@@ -129,13 +130,13 @@ def tile_blockdiagmnistconvertible_pa_t_kernel(tc, x, W1, b1, Wb, bb, out):
         wbg = [wq.tile([P, 2048], BF16, name="wbg%d" % n, align_bytes=64) for n in range(NB)]
         xgs, xcs, hTs, hgs, hcs, zs = {}, {}, {}, {}, {}, {}
 
-        def w1_half(n, h, eng):
+        def w1_half(n, h, eng, bank="T"):
             w32 = w1s[n][:].bitcast(F32).rearrange("p (t q u) -> p t q u", t=4, u=2)
-            transpose_half(lambda t, u: w32[:, t, :, u], w1g[n], h, eng)
+            transpose_half(lambda t, u: w32[:, t, :, u], w1g[n], h, eng, bank)
 
-        def wb_half(n, h, eng):
+        def wb_half(n, h, eng, bank="T"):
             w32 = wbs[n][:].bitcast(F32).rearrange("p (j q u) -> p j q u", j=4, u=2)
-            transpose_half(lambda j, u: w32[:, j, :, u], wbg[n], h, eng)
+            transpose_half(lambda j, u: w32[:, j, :, u], wbg[n], h, eng, bank)
 
         def x_half(c, h, eng="S"):
             if c >= CHUNKS:
@@ -240,92 +241,81 @@ def tile_blockdiagmnistconvertible_pa_t_kernel(tc, x, W1, b1, Wb, bb, out):
         def relu_row(c, r, row, eng):
             if c < 0:
                 return
-            z = zs[(c, r)]
-            relu2(eng, z[:, row * HID : (row + 1) * HID])
+            ap = zs[(c, r)][:, row * HID : (row + 1) * HID]
+            relu2(eng, ap)
+            base = (c * TILES + 2 * r + row) * HID
+            nc.sync.dma_start(out=out_v[:, base : base + HID], in_=ap)
 
-        def store(c, r):
-            if c < 0:
-                return
-            base = c * TILES * HID + r * 2 * HID
-            nc.sync.dma_start(out=out_v[:, base : base + 2 * HID], in_=zs[(c, r)][:])
+        junk = const.tile([P, BLK], BF16, name="junk")
+        nc.vector.memset(junk[:], 0.0)
+        nc.vector.tensor_copy(out=b1f[:], in_=b1b[:])
 
-        def store_row(c, r, row):
-            base = c * TILES * HID + r * 2 * HID + row * HID
-            z = zs[(c, r)]
-            nc.sync.dma_start(
-                out=out_v[:, base : base + HID], in_=z[:, row * HID : (row + 1) * HID]
-            )
+        def warm(count):
+            for i in range(count):
+                acc = ps_s1.tile([P, CW], F32, name="acc1")
+                nc.tensor.matmul(out=acc[:], lhsT=junk[:, :P], rhs=junk[:], start=True, stop=True)
 
+        warm(6)
         x_half(0, 0, "S")
         x_half(0, 1, "V")
-        w1_half(0, 0, "S")
+        w1_half(0, 0, "S", "A")
+        w1_half(0, 1, "V", "A")
         x_quant(0)
-        w1_half(0, 1, "V")
-        w1_half(1, 0, "S")
+        w1_half(1, 0, "S", "A")
+        w1_half(1, 1, "S")
         quantise(w1g[0], w1c[0], w1sc[0])
-        w1_half(1, 1, "V")
-        for t in range(4):
-            s1(0, 0, t, "SV"[t % 2])
-            if t == 0:
-                quantise(w1g[1], w1c[1], w1sc[1])
-        x_half(1, 0, "S")
-        wb_half(0, 0, "V")
-        for t in range(4):
-            s1(0, 1, t, "SV"[t % 2])
-            if t == 0:
-                regroup(0, 0)
-        x_half(1, 1, "S")
-        wb_half(0, 1, "V")
-        x_quant(1)
-        wb_half(1, 0, "S")
-        regroup(0, 1)
-        quantise(wbg[0], wbc[0], wbsc[0])
-        h_quant(0, 0)
-        wb_half(1, 1, "S")
-        spread_bb(0, "S")
+        spread_bb(0, "V")
+        quantise(w1g[1], w1c[1], w1sc[1])
         spread_bb(1, "S")
-        quantise(wbg[1], wbc[1], wbsc[1])
-        h_quant(0, 1)
-        x_half(2, 0)
-        x_half(2, 1)
+        for t in range(4):
+            s1(0, 0, t, "VS"[t % 2])
+        for t in range(3):
+            s1(0, 1, t, "S")
+        regroup(0, 0)
+        x_half(1, 0, "V")
+        h_quant(0, 0)
+        s1(0, 1, 3, "S")
+        x_half(1, 1, "S")
+        wb_half(0, 0, "S", "A")
+        wb_half(0, 1, "S", "A")
+        regroup(0, 1)
+        x_quant(1)
+        wb_half(1, 0, "S", "A")
+        wb_half(1, 1, "S", "A")
         s1(1, 0, 0)
         s1(1, 0, 1)
-        x_quant(2)
+        quantise(wbg[0], wbc[0], wbsc[0])
+        h_quant(0, 1)
+        quantise(wbg[1], wbc[1], wbsc[1])
 
         for c in range(CHUNKS):
             last = c == CHUNKS - 1
             s2(c - 1, 1, 3)
             s1(c + 1, 0, 2)
             relu_row(c - 1, 1, 0, "G")
-            if c > 0:
-                store(c - 1, 1)
             s2(c, 0, 0)
             s1(c + 1, 0, 3)
             s2(c, 0, 1)
-            s1(c + 1, 1, 0)
             s2(c, 0, 2)
-            s1(c + 1, 1, 1)
-            relu_row(c, 0, 1, "S")
+            x_half(c + 2, 0)
+            x_half(c + 2, 1)
+            s1(c + 1, 1, 0)
             regroup(c + 1, 0)
+            s1(c + 1, 1, 1)
+            x_quant(c + 2)
             s1(c + 1, 1, 2)
             s2(c, 0, 3)
-            relu_row(c, 0, 0, "G")
-            store(c, 0)
             s1(c + 1, 1, 3)
+            relu_row(c, 0, 1, "S")
+            relu_row(c, 0, 0, "G")
             s2(c, 1, 0)
             s2(c, 1, 1)
             s2(c, 1, 2)
-            x_half(c + 3, 0)
-            x_half(c + 3, 1)
-            relu_row(c, 1, 1, "S")
-            if last:
-                store_row(c, 1, 1)
             regroup(c + 1, 1)
             h_quant(c + 1, 0)
-            x_quant(c + 3)
             h_quant(c + 1, 1)
             s1(c + 2, 0, 0)
             s1(c + 2, 0, 1)
+            relu_row(c, 1, 1, "S")
         s2(CHUNKS - 1, 1, 3)
         relu_row(CHUNKS - 1, 1, 0, "V")
-        store_row(CHUNKS - 1, 1, 0)

@@ -33,9 +33,10 @@ def tile_blockdiagmnistconvertible_pa_t_kernel(tc, x, W1, b1, Wb, bb, out):
         win = ctx.enter_context(tc.tile_pool(name="win", bufs=1))
         wq = ctx.enter_context(tc.tile_pool(name="wq", bufs=1))
         wgp = ctx.enter_context(tc.tile_pool(name="wgp", bufs=2))
-        xq = ctx.enter_context(tc.tile_pool(name="xq", bufs=4))
+        xq = ctx.enter_context(tc.tile_pool(name="xq", bufs=3))
         hp = ctx.enter_context(tc.tile_pool(name="hp", bufs=4))
-        zp = ctx.enter_context(tc.tile_pool(name="zp", bufs=6))
+        codes = ctx.enter_context(tc.tile_pool(name="codes", bufs=CHUNKS))
+        zp = ctx.enter_context(tc.tile_pool(name="zp", bufs=11))
         ps_tr = ctx.enter_context(tc.psum_pool(name="ps_tr", bufs=2))
         ps_s1 = ctx.enter_context(tc.psum_pool(name="ps_s1", bufs=3))
         ps_s2 = ctx.enter_context(tc.psum_pool(name="ps_s2", bufs=3))
@@ -100,8 +101,7 @@ def tile_blockdiagmnistconvertible_pa_t_kernel(tc, x, W1, b1, Wb, bb, out):
             else:
                 nc.vector.tensor_copy(out=dst, in_=src)
 
-        def transpose_half(src_words, grouped, h, eng, bank="T"):
-            g32 = grouped[:].bitcast(F32).rearrange("p (c u) -> p c u", u=2)
+        def transposes(src_words, h, bank="T"):
             if bank == "T":
                 pt = ps_tr.tile([P, 512], F32, name="pt")
             else:
@@ -113,14 +113,21 @@ def tile_blockdiagmnistconvertible_pa_t_kernel(tc, x, W1, b1, Wb, bb, out):
                         src_words(2 * h + il, u),
                         ident[:],
                     )
+            return pt
+
+        def interleave(pt, grouped, h, eng):
+            g32 = grouped[:].bitcast(F32).rearrange("p (c u) -> p c u", u=2)
             copy_words(
                 eng,
                 g32[:, h * 256 : (h + 1) * 256, :],
                 pt[:].rearrange("p (u c) -> p c u", u=2),
             )
 
-        def quantise(grouped, codes, scales):
-            nc.vector.quantize_mx(out=codes[:].bitcast(FP8X4), scales=scales[:], in_=grouped[:])
+        def transpose_half(src_words, grouped, h, eng, bank="T"):
+            interleave(transposes(src_words, h, bank), grouped, h, eng)
+
+        def quantise(grouped, words, scales):
+            nc.vector.quantize_mx(out=words[:].bitcast(FP8X4), scales=scales[:], in_=grouped[:])
 
         w1c = [wq.tile([P, 512], U32, name="w1c%d" % n, align_bytes=64) for n in range(NB)]
         w1sc = [wq.tile([P, 512], U8, name="w1sc%d" % n, align_bytes=64) for n in range(NB)]
@@ -128,7 +135,7 @@ def tile_blockdiagmnistconvertible_pa_t_kernel(tc, x, W1, b1, Wb, bb, out):
         wbsc = [wq.tile([P, 512], U8, name="wbsc%d" % n, align_bytes=64) for n in range(NB)]
         w1g = [wq.tile([P, 2048], BF16, name="w1g%d" % n, align_bytes=64) for n in range(NB)]
         wbg = [wq.tile([P, 2048], BF16, name="wbg%d" % n, align_bytes=64) for n in range(NB)]
-        xgs, xcs, hTs, hgs, hcs, zs = {}, {}, {}, {}, {}, {}
+        xgs, xcs, hTs, hgs, hcs, zs, acc1s, acc2s, xps = {}, {}, {}, {}, {}, {}, {}, {}, {}
 
         def w1_half(n, h, eng, bank="T"):
             w32 = w1s[n][:].bitcast(F32).rearrange("p (t q u) -> p t q u", t=4, u=2)
@@ -138,29 +145,37 @@ def tile_blockdiagmnistconvertible_pa_t_kernel(tc, x, W1, b1, Wb, bb, out):
             w32 = wbs[n][:].bitcast(F32).rearrange("p (j q u) -> p j q u", j=4, u=2)
             transpose_half(lambda j, u: w32[:, j, :, u], wbg[n], h, eng, bank)
 
-        def x_half(c, h, eng="S"):
+        def x_tr(c, halves=(0, 1)):
             if c >= CHUNKS:
                 return
-            if h == 0:
+            x32 = xs[c][:].bitcast(F32).rearrange("p (i q u) -> p i q u", i=TILES, u=2)
+            for h in halves:
+                xps[(c, h)] = transposes(lambda i, u: x32[:, i, :, u], h)
+
+        def x_copy(c, halves=(0, 1), eng="S"):
+            if c >= CHUNKS:
+                return
+            if halves[0] == 0:
                 xg = xq.tile([P, 2048], BF16, name="xg", align_bytes=64)
                 xgs[c] = xg
-            x32 = xs[c][:].bitcast(F32).rearrange("p (i q u) -> p i q u", i=TILES, u=2)
-            transpose_half(lambda i, u: x32[:, i, :, u], xgs[c], h, eng)
+            for h in halves:
+                interleave(xps[(c, h)], xgs[c], h, eng)
+
+        def x_half(c, h, eng="S"):
+            x_tr(c, (h,))
+            x_copy(c, (h,), eng)
 
         def x_quant(c):
             if c >= CHUNKS:
                 return
-            xc = xq.tile([P, CW], U32, name="xc", align_bytes=64)
-            xsc = xq.tile([P, CW], U8, name="xsc", align_bytes=64)
+            xc = codes.tile([P, CW], U32, name="xc", align_bytes=64)
+            xsc = codes.tile([P, CW], U8, name="xsc", align_bytes=64)
             quantise(xgs[c], xc, xsc)
             xcs[c] = (xc, xsc)
 
-        def s1(c, n, t, eng="S"):
+        def s1_mm(c, n, t):
             if c >= CHUNKS:
                 return
-            if t == 0:
-                hT = hp.tile([P, 4 * CW], BF16, name="hT")
-                hTs[(c, n)] = hT
             xc, xsc = xcs[c]
             acc = ps_s1.tile([P, CW], F32, name="acc1")
             nc.tensor.matmul_mx(
@@ -172,6 +187,15 @@ def tile_blockdiagmnistconvertible_pa_t_kernel(tc, x, W1, b1, Wb, bb, out):
                 start=True,
                 stop=True,
             )
+            acc1s[(c, n, t)] = acc
+
+        def s1_act(c, n, t, eng="S"):
+            if c >= CHUNKS:
+                return
+            if t == 0:
+                hT = hp.tile([P, 4 * CW], BF16, name="hT")
+                hTs[(c, n)] = hT
+            acc = acc1s[(c, n, t)]
             dst = hTs[(c, n)][:, t * CW : (t + 1) * CW]
             bias = b1f[:, 4 * n + t : 4 * n + t + 1]
             if eng == "S":
@@ -181,21 +205,25 @@ def tile_blockdiagmnistconvertible_pa_t_kernel(tc, x, W1, b1, Wb, bb, out):
                     out=dst, in0=acc[:], scalar1=bias, scalar2=0.0, op0=ALU.add, op1=ALU.max
                 )
 
-        def regroup(c, n):
+        def s1(c, n, t, eng="S"):
+            s1_mm(c, n, t)
+            s1_act(c, n, t, eng)
+
+        def regroup(c, n, eng="V", lo=0, hi=CW):
             if c >= CHUNKS:
                 return
-            hg = hp.tile([P, 4 * CW], BF16, name="hg", align_bytes=64)
-            nc.vector.tensor_copy(
-                out=hg[:].rearrange("p (c i t) -> p c t i", i=4, t=4),
-                in_=hTs[(c, n)][:].rearrange("p (t c i) -> p c t i", t=4, i=4),
-            )
-            hgs[(c, n)] = hg
+            if lo == 0:
+                hg = hp.tile([P, 4 * CW], BF16, name="hg", align_bytes=64)
+                hgs[(c, n)] = hg
+            dst = hgs[(c, n)][:].rearrange("p (c i t) -> p c t i", i=4, t=4)
+            src = hTs[(c, n)][:].rearrange("p (t c i) -> p c t i", t=4, i=4)
+            copy_words(eng, dst[:, lo // 4 : hi // 4], src[:, lo // 4 : hi // 4])
 
         def h_quant(c, n):
             if c >= CHUNKS:
                 return
-            hc = hp.tile([P, CW], U32, name="hc%d" % n, align_bytes=64)
-            hsc = hp.tile([P, CW], U8, name="hsc%d" % n, align_bytes=64)
+            hc = codes.tile([P, CW], U32, name="hc%d" % n, align_bytes=64)
+            hsc = codes.tile([P, CW], U8, name="hsc%d" % n, align_bytes=64)
             quantise(hgs[(c, n)], hc, hsc)
             hcs[(c, n)] = (hc, hsc)
 
@@ -209,17 +237,10 @@ def tile_blockdiagmnistconvertible_pa_t_kernel(tc, x, W1, b1, Wb, bb, out):
                     out=ap, in0=ap, scalar1=F32_MAX, scalar2=0.0, op0=ALU.min, op1=ALU.max
                 )
 
-        ADDS = ((1, 0), (1, 1), (0, 1), (0, 0))
-
-        def s2(c, r, j):
-            if c < 0:
+        def s2_mm(c, k):
+            if c >= CHUNKS:
                 return
-            row, n = ADDS[j]
-            if j == 0:
-                z = zp.tile([P, 2 * HID], F32, name="z")
-                zs[(c, r)] = z
-            z = zs[(c, r)]
-            il = 2 * r + row
+            il, n = divmod(k, NB)
             hc, hsc = hcs[(c, n)]
             acc = ps_s2.tile([P, BLK], F32, name="acc2")
             nc.tensor.matmul_mx(
@@ -231,20 +252,27 @@ def tile_blockdiagmnistconvertible_pa_t_kernel(tc, x, W1, b1, Wb, bb, out):
                 start=True,
                 stop=True,
             )
+            acc2s[(c, k)] = acc
+
+        def s2_add(c, k):
+            il, n = divmod(k, NB)
+            if n == 0:
+                z = zp.tile([P, HID], F32, name="z")
+                zs[(c, il)] = z
+            z = zs[(c, il)]
+            acc = acc2s[(c, k)]
             nc.vector.tensor_tensor(
-                out=z[:, row * HID + n * BLK : row * HID + (n + 1) * BLK],
+                out=z[:, n * BLK : (n + 1) * BLK],
                 in0=acc[:],
                 in1=bbb[:, n * BLK : (n + 1) * BLK],
                 op=ALU.add,
             )
 
-        def relu_row(c, r, row, eng):
-            if c < 0:
-                return
-            ap = zs[(c, r)][:, row * HID : (row + 1) * HID]
+        def finish(c, il, eng, lo=0, hi=HID):
+            ap = zs[(c, il)][:, lo:hi]
             relu2(eng, ap)
-            base = (c * TILES + 2 * r + row) * HID
-            nc.sync.dma_start(out=out_v[:, base : base + HID], in_=ap)
+            base = (c * TILES + il) * HID
+            nc.sync.dma_start(out=out_v[:, base + lo : base + hi], in_=ap)
 
         junk = const.tile([P, BLK], BF16, name="junk")
         nc.vector.memset(junk[:], 0.0)
@@ -282,40 +310,70 @@ def tile_blockdiagmnistconvertible_pa_t_kernel(tc, x, W1, b1, Wb, bb, out):
         x_quant(1)
         wb_half(1, 0, "S", "A")
         wb_half(1, 1, "S", "A")
-        s1(1, 0, 0)
-        s1(1, 0, 1)
+        for t in range(3):
+            s1_mm(1, 0, t)
+        s1_act(1, 0, 0)
         quantise(wbg[0], wbc[0], wbsc[0])
         h_quant(0, 1)
         quantise(wbg[1], wbc[1], wbsc[1])
+        x_tr(2)
+        s2_mm(0, 0)
+        s1_mm(1, 0, 3)
+        s1_act(1, 0, 1)
+        s1_mm(1, 1, 0)
+        s2_mm(0, 1)
+        s1_act(1, 0, 2)
+        s1_mm(1, 1, 1)
+        s1_act(1, 0, 3)
+        s1_mm(1, 1, 2)
 
         for c in range(CHUNKS):
             last = c == CHUNKS - 1
-            s2(c - 1, 1, 3)
-            s1(c + 1, 0, 2)
-            relu_row(c - 1, 1, 0, "G")
-            s2(c, 0, 0)
-            s1(c + 1, 0, 3)
-            s2(c, 0, 1)
-            s2(c, 0, 2)
-            x_half(c + 2, 0)
-            x_half(c + 2, 1)
-            s1(c + 1, 1, 0)
-            regroup(c + 1, 0)
-            s1(c + 1, 1, 1)
+            if c > 0:
+                s2_add(c - 1, 7)
+            s2_mm(c, 2)
+            if c > 0:
+                finish(c - 1, 3, "G")
+            s1_act(c + 1, 1, 0)
+            s1_mm(c + 1, 1, 3)
+            s2_add(c, 0)
+            s2_mm(c, 3)
+            s1_act(c + 1, 1, 1)
+            s2_add(c, 1)
+            s2_mm(c, 4)
+            finish(c, 0, "G")
+            s1_act(c + 1, 1, 2)
+            s1_act(c + 1, 1, 3)
+            s2_add(c, 2)
+            s2_mm(c, 5)
+            x_copy(c + 2)
+            s2_add(c, 3)
+            s2_mm(c, 6)
+            finish(c, 1, "S")
+            s2_add(c, 4)
+            s2_mm(c, 7)
+            s2_add(c, 5)
+            finish(c, 2, "S")
+            s2_add(c, 6)
+            if last:
+                finish(c, 3, "S", 0, BLK)
             x_quant(c + 2)
-            s1(c + 1, 1, 2)
-            s2(c, 0, 3)
-            s1(c + 1, 1, 3)
-            relu_row(c, 0, 1, "S")
-            relu_row(c, 0, 0, "G")
-            s2(c, 1, 0)
-            s2(c, 1, 1)
-            s2(c, 1, 2)
+            x_tr(c + 3)
+            for t in range(3):
+                s1_mm(c + 2, 0, t)
+            regroup(c + 1, 0)
+            s1_act(c + 2, 0, 0)
+            s1_mm(c + 2, 0, 3)
+            s1_act(c + 2, 0, 1)
+            s1_mm(c + 2, 1, 0)
             regroup(c + 1, 1)
+            s1_act(c + 2, 0, 2)
+            s1_mm(c + 2, 1, 1)
             h_quant(c + 1, 0)
+            s2_mm(c + 1, 0)
+            s1_act(c + 2, 0, 3)
+            s1_mm(c + 2, 1, 2)
             h_quant(c + 1, 1)
-            s1(c + 2, 0, 0)
-            s1(c + 2, 0, 1)
-            relu_row(c, 1, 1, "S")
-        s2(CHUNKS - 1, 1, 3)
-        relu_row(CHUNKS - 1, 1, 0, "V")
+            s2_mm(c + 1, 1)
+        s2_add(CHUNKS - 1, 7)
+        finish(CHUNKS - 1, 3, "V", BLK, HID)

@@ -196,7 +196,11 @@ def tile_blockdiagmnistconvertible_pa_t_kernel(tc, x, W1, b1, Wb, bb, out):
                 hT = hp.tile([P, 4 * CW], BF16, name="hT")
                 hTs[(c, n)] = hT
             acc = acc1s[(c, n, t)]
-            dst = hTs[(c, n)][:, t * CW : (t + 1) * CW]
+            hT = hTs[(c, n)]
+            if paired(c, n):
+                dst = hT[:].rearrange("p (u c e) -> p u e c", u=2, e=2)[:, t // 2, t % 2]
+            else:
+                dst = hT[:, t * CW : (t + 1) * CW]
             bias = b1f[:, 4 * n + t : 4 * n + t + 1]
             if eng == "S":
                 nc.scalar.activation(out=dst, in_=acc[:], func=ACT.Relu, bias=bias, scale=1.0)
@@ -209,15 +213,24 @@ def tile_blockdiagmnistconvertible_pa_t_kernel(tc, x, W1, b1, Wb, bb, out):
             s1_mm(c, n, t)
             s1_act(c, n, t, eng)
 
-        def regroup(c, n, eng="V", lo=0, hi=CW):
+        def paired(c, n):
+            return c > 0 and n == 1
+
+        def regroup(c, n, eng="V"):
             if c >= CHUNKS:
                 return
-            if lo == 0:
-                hg = hp.tile([P, 4 * CW], BF16, name="hg", align_bytes=64)
-                hgs[(c, n)] = hg
+            hg = hp.tile([P, 4 * CW], BF16, name="hg", align_bytes=64)
+            hgs[(c, n)] = hg
+            if paired(c, n):
+                copy_words(
+                    eng,
+                    hg[:].bitcast(F32).rearrange("p (c i u) -> p c u i", i=2, u=2),
+                    hTs[(c, n)][:].bitcast(F32).rearrange("p (u c i) -> p c u i", u=2, i=2),
+                )
+                return
             dst = hgs[(c, n)][:].rearrange("p (c i t) -> p c t i", i=4, t=4)
             src = hTs[(c, n)][:].rearrange("p (t c i) -> p c t i", t=4, i=4)
-            copy_words(eng, dst[:, lo // 4 : hi // 4], src[:, lo // 4 : hi // 4])
+            copy_words(eng, dst, src)
 
         def h_quant(c, n):
             if c >= CHUNKS:
@@ -334,22 +347,22 @@ def tile_blockdiagmnistconvertible_pa_t_kernel(tc, x, W1, b1, Wb, bb, out):
             s2_mm(c, 2)
             if c > 0:
                 finish(c - 1, 3, "G")
+            x_copy(c + 2)
             s1_act(c + 1, 1, 0)
-            s1_mm(c + 1, 1, 3)
             s2_add(c, 0)
             s2_mm(c, 3)
             s1_act(c + 1, 1, 1)
             s2_add(c, 1)
             s2_mm(c, 4)
+            s1_mm(c + 1, 1, 3)
             finish(c, 0, "G")
             s1_act(c + 1, 1, 2)
             s1_act(c + 1, 1, 3)
             s2_add(c, 2)
             s2_mm(c, 5)
-            x_copy(c + 2)
             s2_add(c, 3)
             s2_mm(c, 6)
-            finish(c, 1, "S")
+            finish(c, 1, "S" if last else "G")
             s2_add(c, 4)
             s2_mm(c, 7)
             s2_add(c, 5)

@@ -29,14 +29,14 @@ def tile_blockdiagmnistconvertible_pa_t_kernel(tc, x, W1, b1, Wb, bb, out):
     nc = tc.nc
     with ExitStack() as ctx:
         const = ctx.enter_context(tc.tile_pool(name="const", bufs=1))
-        xin = ctx.enter_context(tc.tile_pool(name="xin", bufs=1))
+        rows = ctx.enter_context(tc.tile_pool(name="rows", bufs=30))
         win = ctx.enter_context(tc.tile_pool(name="win", bufs=1))
         wq = ctx.enter_context(tc.tile_pool(name="wq", bufs=1))
         wgp = ctx.enter_context(tc.tile_pool(name="wgp", bufs=2))
         xq = ctx.enter_context(tc.tile_pool(name="xq", bufs=3))
         hp = ctx.enter_context(tc.tile_pool(name="hp", bufs=4))
-        codes = ctx.enter_context(tc.tile_pool(name="codes", bufs=CHUNKS))
-        zp = ctx.enter_context(tc.tile_pool(name="zp", bufs=11))
+        gp = ctx.enter_context(tc.tile_pool(name="gp", bufs=3))
+        codes = ctx.enter_context(tc.tile_pool(name="codes", bufs=3))
         ps_tr = ctx.enter_context(tc.psum_pool(name="ps_tr", bufs=2))
         ps_s1 = ctx.enter_context(tc.psum_pool(name="ps_s1", bufs=3))
         ps_s2 = ctx.enter_context(tc.psum_pool(name="ps_s2", bufs=3))
@@ -47,18 +47,24 @@ def tile_blockdiagmnistconvertible_pa_t_kernel(tc, x, W1, b1, Wb, bb, out):
 
         xs = []
         for c in range(CHUNKS):
-            xs.append(xin.tile([P, TILES * IN], BF16, name="xs%d" % c))
+            row = rows.tile([P, TILES * IN], BF16, name="row")
+            xs.append(row)
         w1s = [win.tile([P, 4 * IN], BF16, name="w1s%d" % n) for n in range(NB)]
         wbs = [win.tile([P, 4 * BLK], BF16, name="wbs%d" % n) for n in range(NB)]
 
-        def load_x(c):
-            nc.sync.dma_start(out=xs[c][:], in_=x_v[:, c * TILES * IN : (c + 1) * TILES * IN])
+        def load_x(c, parts=1):
+            w = TILES * IN // parts
+            for h in range(parts):
+                lo = c * TILES * IN + h * w
+                nc.sync.dma_start(out=xs[c][:, h * w : (h + 1) * w], in_=x_v[:, lo : lo + w])
 
-        def load_w1(n):
-            nc.sync.dma_start(
-                out=w1s[n][:],
-                in_=W1[n * BLK : (n + 1) * BLK, :].rearrange("(p t) k -> p (t k)", t=4),
-            )
+        def load_w1(n, parts=1):
+            src = W1[n * BLK : (n + 1) * BLK, :].rearrange("(p t) k -> p (t k)", t=4)
+            w = 4 * IN // parts
+            for h in range(parts):
+                nc.sync.dma_start(
+                    out=w1s[n][:, h * w : (h + 1) * w], in_=src[:, h * w : (h + 1) * w]
+                )
 
         def load_wb(n):
             nc.sync.dma_start(
@@ -68,33 +74,22 @@ def tile_blockdiagmnistconvertible_pa_t_kernel(tc, x, W1, b1, Wb, bb, out):
 
         b1b = const.tile([P, 2 * 4], BF16, name="b1b")
         b1f = const.tile([P, 2 * 4], F32, name="b1f")
-        bbrow = const.tile([P, HID], BF16, name="bbrow")
-        ones = const.tile([P, P], BF16, name="ones")
-        bbb = const.tile([P, HID], F32, name="bbb")
+        bbb = const.tile([P, HID], BF16, name="bbb")
         ident = const.tile([P, P], F32, name="ident")
         nc.scalar.dma_start(
             out=b1b[:].rearrange("p (n t) -> p n t", t=4),
             in_=b1.rearrange("(n p t) -> p n t", n=NB, t=4),
         )
         make_identity(nc, ident[:])
-        nc.gpsimd.memset(bbrow[:], 0.0)
-        nc.gpsimd.memset(ones[:], 1.0)
-        load_x(0)
-        load_w1(0)
+        load_x(0, 2)
+        load_w1(0, 2)
         load_w1(1)
-        nc.sync.dma_start(out=bbrow[0:1, :], in_=bb.rearrange("(o n) -> o n", o=1))
         load_x(1)
         load_wb(0)
         load_wb(1)
+        nc.sync.dma_start(out=bbb[:], in_=bb.partition_broadcast(P))
         for c in range(2, CHUNKS):
             load_x(c)
-        def spread_bb(n, eng):
-            pb = ps_s1.tile([P, CW], F32, name="acc1")
-            nc.tensor.matmul(
-                out=pb[:], lhsT=ones[:], rhs=bbrow[:, n * BLK : (n + 1) * BLK], start=True, stop=True
-            )
-            copy_words(eng, bbb[:, n * BLK : (n + 1) * BLK], pb[:])
-
         def copy_words(eng, dst, src):
             if eng == "S":
                 nc.scalar.copy(out=dst, in_=src)
@@ -214,12 +209,12 @@ def tile_blockdiagmnistconvertible_pa_t_kernel(tc, x, W1, b1, Wb, bb, out):
             s1_act(c, n, t, eng)
 
         def paired(c, n):
-            return c > 0 and n == 1
+            return c > 1 and n == 1
 
         def regroup(c, n, eng="V"):
             if c >= CHUNKS:
                 return
-            hg = hp.tile([P, 4 * CW], BF16, name="hg", align_bytes=64)
+            hg = gp.tile([P, 4 * CW], BF16, name="hg", align_bytes=64)
             hgs[(c, n)] = hg
             if paired(c, n):
                 copy_words(
@@ -270,8 +265,8 @@ def tile_blockdiagmnistconvertible_pa_t_kernel(tc, x, W1, b1, Wb, bb, out):
         def s2_add(c, k):
             il, n = divmod(k, NB)
             if n == 0:
-                z = zp.tile([P, HID], F32, name="z")
-                zs[(c, il)] = z
+                row = rows.tile([P, HID], F32, name="row")
+                zs[(c, il)] = row
             z = zs[(c, il)]
             acc = acc2s[(c, k)]
             nc.vector.tensor_tensor(
@@ -296,7 +291,7 @@ def tile_blockdiagmnistconvertible_pa_t_kernel(tc, x, W1, b1, Wb, bb, out):
                 acc = ps_s1.tile([P, CW], F32, name="acc1")
                 nc.tensor.matmul(out=acc[:], lhsT=junk[:, :P], rhs=junk[:], start=True, stop=True)
 
-        warm(6)
+        warm(4)
         x_half(0, 0, "S")
         x_half(0, 1, "V")
         w1_half(0, 0, "S", "A")
@@ -305,9 +300,7 @@ def tile_blockdiagmnistconvertible_pa_t_kernel(tc, x, W1, b1, Wb, bb, out):
         w1_half(1, 0, "S", "A")
         w1_half(1, 1, "S")
         quantise(w1g[0], w1c[0], w1sc[0])
-        spread_bb(0, "V")
         quantise(w1g[1], w1c[1], w1sc[1])
-        spread_bb(1, "S")
         for t in range(4):
             s1(0, 0, t, "VS"[t % 2])
         for t in range(3):
@@ -323,70 +316,98 @@ def tile_blockdiagmnistconvertible_pa_t_kernel(tc, x, W1, b1, Wb, bb, out):
         x_quant(1)
         wb_half(1, 0, "S", "A")
         wb_half(1, 1, "S", "A")
-        for t in range(3):
-            s1_mm(1, 0, t)
-        s1_act(1, 0, 0)
         quantise(wbg[0], wbc[0], wbsc[0])
         h_quant(0, 1)
         quantise(wbg[1], wbc[1], wbsc[1])
-        x_tr(2)
+        s1_mm(1, 0, 0)
+        s1_mm(1, 0, 1)
         s2_mm(0, 0)
+        s1_mm(1, 0, 2)
+        s2_mm(0, 1)
+        s1_act(1, 0, 0)
+        s2_mm(0, 2)
         s1_mm(1, 0, 3)
         s1_act(1, 0, 1)
-        s1_mm(1, 1, 0)
-        s2_mm(0, 1)
         s1_act(1, 0, 2)
-        s1_mm(1, 1, 1)
         s1_act(1, 0, 3)
-        s1_mm(1, 1, 2)
 
         for c in range(CHUNKS):
+            first = c == 0
             last = c == CHUNKS - 1
-            if c > 0:
-                s2_add(c - 1, 7)
-            s2_mm(c, 2)
-            if c > 0:
-                finish(c - 1, 3, "G")
-            x_copy(c + 2)
-            s1_act(c + 1, 1, 0)
+            if not first:
+                x_copy(c + 3)
+                s1_act(c + 1, 1, 0)
             s2_add(c, 0)
             s2_mm(c, 3)
-            s1_act(c + 1, 1, 1)
+            if first:
+                s1_mm(1, 1, 0)
             s2_add(c, 1)
             s2_mm(c, 4)
-            s1_mm(c + 1, 1, 3)
+            if first:
+                s1_mm(1, 1, 1)
+                s1_mm(1, 1, 2)
+                s1_act(1, 1, 0)
             finish(c, 0, "G")
-            s1_act(c + 1, 1, 2)
-            s1_act(c + 1, 1, 3)
             s2_add(c, 2)
             s2_mm(c, 5)
+            s1_act(c + 1, 1, 1)
             s2_add(c, 3)
             s2_mm(c, 6)
             finish(c, 1, "S" if last else "G")
+            s1_act(c + 1, 1, 2)
             s2_add(c, 4)
             s2_mm(c, 7)
-            s2_add(c, 5)
-            finish(c, 2, "S")
-            s2_add(c, 6)
-            if last:
-                finish(c, 3, "S", 0, BLK)
-            x_quant(c + 2)
-            x_tr(c + 3)
-            for t in range(3):
-                s1_mm(c + 2, 0, t)
-            regroup(c + 1, 0)
-            s1_act(c + 2, 0, 0)
-            s1_mm(c + 2, 0, 3)
-            s1_act(c + 2, 0, 1)
-            s1_mm(c + 2, 1, 0)
-            regroup(c + 1, 1)
-            s1_act(c + 2, 0, 2)
-            s1_mm(c + 2, 1, 1)
+            if first:
+                s1_mm(1, 1, 3)
+                x_tr(2)
+                s1_act(1, 1, 3)
+                s2_add(0, 5)
+                x_copy(2)
+                x_tr(3)
+                s2_add(0, 6)
+                regroup(1, 0)
+                regroup(1, 1)
+                x_quant(2)
+                for t in range(3):
+                    s1_mm(2, 0, t)
+                finish(0, 2, "V")
+                x_copy(3)
+            else:
+                s1_mm(c + 1, 1, 3)
+                s1_mm(c + 2, 0, 0)
+                x_tr(c + 4)
+                s1_mm(c + 2, 0, 1)
+                s1_act(c + 1, 1, 3)
+                s2_add(c, 5)
+                finish(c, 2, "S")
+                s1_mm(c + 2, 0, 2)
+                s2_add(c, 6)
+                if last:
+                    finish(c, 3, "S", 0, BLK)
+                regroup(c + 1, 0)
+                regroup(c + 1, 1)
             h_quant(c + 1, 0)
             s2_mm(c + 1, 0)
+            s1_act(c + 2, 0, 0)
+            s1_mm(c + 2, 0, 3)
+            h_quant(c + 1, 1)
+            s1_act(c + 2, 0, 1)
+            if not first:
+                s1_mm(c + 2, 1, 0)
+            s2_mm(c + 1, 1)
+            s1_act(c + 2, 0, 2)
+            if not first:
+                s1_mm(c + 2, 1, 1)
+            s2_add(c, 7)
+            s2_mm(c + 1, 2)
+            if first:
+                x_tr(4)
+                s1_mm(2, 1, 0)
+                s1_mm(2, 1, 1)
+            if last:
+                finish(c, 3, "V", BLK, HID)
+            else:
+                finish(c, 3, "G")
+            x_quant(c + 3)
             s1_act(c + 2, 0, 3)
             s1_mm(c + 2, 1, 2)
-            h_quant(c + 1, 1)
-            s2_mm(c + 1, 1)
-        s2_add(CHUNKS - 1, 7)
-        finish(CHUNKS - 1, 3, "V", BLK, HID)

@@ -209,7 +209,7 @@ def tile_blockdiagmnistconvertible_pa_t_kernel(tc, x, W1, b1, Wb, bb, out):
             s1_act(c, n, t, eng)
 
         def paired(c, n):
-            return c > 1 and n == 1
+            return c > 1 and n == 1 or c == CHUNKS - 1
 
         def regroup(c, n, eng="V"):
             if c >= CHUNKS:
@@ -276,15 +276,22 @@ def tile_blockdiagmnistconvertible_pa_t_kernel(tc, x, W1, b1, Wb, bb, out):
                 op=ALU.add,
             )
 
-        def finish(c, il, eng, lo=0, hi=HID):
-            ap = zs[(c, il)][:, lo:hi]
-            relu2(eng, ap)
+        def relu_part(c, il, eng, lo, hi):
+            relu2(eng, zs[(c, il)][:, lo:hi])
+
+        def finish(c, il, eng, lo=0, hi=HID, relu_hi=None):
+            relu2(eng, zs[(c, il)][:, lo : relu_hi or hi])
             base = (c * TILES + il) * HID
-            nc.sync.dma_start(out=out_v[:, base + lo : base + hi], in_=ap)
+            nc.sync.dma_start(out=out_v[:, base + lo : base + hi], in_=zs[(c, il)][:, lo:hi])
 
         junk = const.tile([P, BLK], BF16, name="junk")
         nc.vector.memset(junk[:], 0.0)
         nc.vector.tensor_copy(out=b1f[:], in_=b1b[:])
+
+        def warm_tr(count):
+            for i in range(count):
+                pt = ps_tr.tile([P, 512], F32, name="pt")
+                nc.tensor.matmul(out=pt[:], lhsT=junk[:, :P], rhs=junk[:], start=True, stop=True)
 
         def warm(count):
             for i in range(count):
@@ -294,15 +301,17 @@ def tile_blockdiagmnistconvertible_pa_t_kernel(tc, x, W1, b1, Wb, bb, out):
         warm(4)
         x_half(0, 0, "S")
         x_half(0, 1, "V")
-        w1_half(0, 0, "S", "A")
-        w1_half(0, 1, "V", "A")
+        w1_half(0, 0, "V", "A")
+        w1_half(0, 1, "S", "A")
         x_quant(0)
-        w1_half(1, 0, "S", "A")
-        w1_half(1, 1, "S")
         quantise(w1g[0], w1c[0], w1sc[0])
+        w1_half(1, 0, "V", "A")
+        w1_half(1, 1, "S")
+        s1(0, 0, 0, "V")
         quantise(w1g[1], w1c[1], w1sc[1])
-        for t in range(4):
-            s1(0, 0, t, "VS"[t % 2])
+        s1(0, 0, 1, "S")
+        s1(0, 0, 2, "V")
+        s1(0, 0, 3, "S")
         for t in range(3):
             s1(0, 1, t, "S")
         regroup(0, 0)
@@ -320,10 +329,10 @@ def tile_blockdiagmnistconvertible_pa_t_kernel(tc, x, W1, b1, Wb, bb, out):
         h_quant(0, 1)
         quantise(wbg[1], wbc[1], wbsc[1])
         s1_mm(1, 0, 0)
-        s1_mm(1, 0, 1)
         s2_mm(0, 0)
-        s1_mm(1, 0, 2)
+        s1_mm(1, 0, 1)
         s2_mm(0, 1)
+        s1_mm(1, 0, 2)
         s1_act(1, 0, 0)
         s2_mm(0, 2)
         s1_mm(1, 0, 3)
@@ -331,83 +340,122 @@ def tile_blockdiagmnistconvertible_pa_t_kernel(tc, x, W1, b1, Wb, bb, out):
         s1_act(1, 0, 2)
         s1_act(1, 0, 3)
 
-        for c in range(CHUNKS):
-            first = c == 0
+        s2_add(0, 0)
+        s2_mm(0, 3)
+        s1_mm(1, 1, 0)
+        s2_add(0, 1)
+        s2_mm(0, 4)
+        s1_mm(1, 1, 1)
+        s1_mm(1, 1, 2)
+        s1_act(1, 1, 0)
+        finish(0, 0, "G")
+        s2_add(0, 2)
+        s2_mm(0, 5)
+        s1_act(1, 1, 1)
+        s2_add(0, 3)
+        s2_mm(0, 6)
+        finish(0, 1, "G")
+        s1_act(1, 1, 2)
+        s2_add(0, 4)
+        s2_mm(0, 7)
+        s1_mm(1, 1, 3)
+        x_tr(2)
+        s1_act(1, 1, 3)
+        s2_add(0, 5)
+        x_copy(2)
+        x_tr(3)
+        s2_add(0, 6)
+        s2_add(0, 7)
+        regroup(1, 0)
+        x_quant(2)
+        regroup(1, 1)
+        for t in range(3):
+            s1_mm(2, 0, t)
+        x_copy(3)
+        h_quant(1, 0)
+        s1_act(2, 0, 0)
+        s2_mm(1, 0)
+        h_quant(1, 1)
+        s1_act(2, 0, 1)
+        s2_mm(1, 1)
+        s2_mm(1, 2)
+        s1_mm(2, 0, 3)
+        s1_act(2, 0, 2)
+        finish(0, 2, "S")
+        x_tr(4)
+        s1_mm(2, 1, 0)
+        s1_mm(2, 1, 1)
+        relu_part(0, 3, "V", 896, HID)
+        finish(0, 3, "G", 0, HID, 900)
+        x_quant(3)
+        s1_act(2, 0, 3)
+
+        for c in range(1, CHUNKS):
             last = c == CHUNKS - 1
-            if not first:
-                x_copy(c + 3)
-                s1_act(c + 1, 1, 0)
+            x_copy(c + 3)
+            s1_act(c + 1, 1, 0)
             s2_add(c, 0)
             s2_mm(c, 3)
-            if first:
-                s1_mm(1, 1, 0)
             s2_add(c, 1)
             s2_mm(c, 4)
-            if first:
-                s1_mm(1, 1, 1)
-                s1_mm(1, 1, 2)
-                s1_act(1, 1, 0)
-            finish(c, 0, "G")
+            s1_mm(c + 1, 1, 2)
+            if last:
+                finish(c, 0, "S", 0, BLK)
+                finish(c, 0, "G", BLK, HID)
+            else:
+                finish(c, 0, "G")
             s2_add(c, 2)
             s2_mm(c, 5)
             s1_act(c + 1, 1, 1)
             s2_add(c, 3)
             s2_mm(c, 6)
-            finish(c, 1, "S" if last else "G")
+            s1_mm(c + 1, 1, 3)
+            if last:
+                finish(c, 1, "S", 0, BLK)
+                finish(c, 1, "G", BLK, HID)
+            else:
+                finish(c, 1, "G")
             s1_act(c + 1, 1, 2)
             s2_add(c, 4)
             s2_mm(c, 7)
-            if first:
-                s1_mm(1, 1, 3)
-                x_tr(2)
-                s1_act(1, 1, 3)
-                s2_add(0, 5)
-                x_copy(2)
-                x_tr(3)
-                s2_add(0, 6)
-                regroup(1, 0)
-                regroup(1, 1)
-                x_quant(2)
-                for t in range(3):
-                    s1_mm(2, 0, t)
-                finish(0, 2, "V")
-                x_copy(3)
+            s1_mm(c + 2, 0, 0)
+            if c + 4 >= CHUNKS:
+                warm_tr(2)
+            x_tr(c + 4)
+            s1_mm(c + 2, 0, 1)
+            s1_act(c + 1, 1, 3)
+            s2_add(c, 5)
+            if last:
+                finish(c, 2, "S", 0, BLK)
+                finish(c, 2, "G", BLK, HID)
             else:
-                s1_mm(c + 1, 1, 3)
-                s1_mm(c + 2, 0, 0)
-                x_tr(c + 4)
-                s1_mm(c + 2, 0, 1)
-                s1_act(c + 1, 1, 3)
-                s2_add(c, 5)
                 finish(c, 2, "S")
-                s1_mm(c + 2, 0, 2)
-                s2_add(c, 6)
-                if last:
-                    finish(c, 3, "S", 0, BLK)
-                regroup(c + 1, 0)
-                regroup(c + 1, 1)
+            s1_mm(c + 2, 0, 2)
+            s2_add(c, 6)
+            if last:
+                finish(c, 3, "S", 0, BLK)
+            s2_add(c, 7)
+            regroup(c + 1, 0)
+            regroup(c + 1, 1)
             h_quant(c + 1, 0)
-            s2_mm(c + 1, 0)
             s1_act(c + 2, 0, 0)
             s1_mm(c + 2, 0, 3)
+            s2_mm(c + 1, 0)
             h_quant(c + 1, 1)
             s1_act(c + 2, 0, 1)
-            if not first:
-                s1_mm(c + 2, 1, 0)
             s2_mm(c + 1, 1)
-            s1_act(c + 2, 0, 2)
-            if not first:
-                s1_mm(c + 2, 1, 1)
-            s2_add(c, 7)
             s2_mm(c + 1, 2)
-            if first:
-                x_tr(4)
-                s1_mm(2, 1, 0)
-                s1_mm(2, 1, 1)
+            s1_act(c + 2, 0, 2)
+            s1_mm(c + 2, 1, 0)
+            s1_mm(c + 2, 1, 1)
             if last:
                 finish(c, 3, "V", BLK, HID)
             else:
-                finish(c, 3, "G")
+                relu_part(c, 3, "V", 896, HID)
+                if c == CHUNKS - 2:
+                    finish(c, 3, "S", 0, BLK)
+                    finish(c, 3, "G", BLK, HID, 900)
+                else:
+                    finish(c, 3, "G", 0, HID, 900)
             x_quant(c + 3)
             s1_act(c + 2, 0, 3)
-            s1_mm(c + 2, 1, 2)

@@ -168,11 +168,14 @@ def tile_blockdiagmnistconvertible_pa_t_kernel(tc, x, W1, b1, Wb, bb, out):
             quantise(xgs[c], xc, xsc)
             xcs[c] = (xc, xsc)
 
-        def s1_mm(c, n, t):
+        def s1_mm(c, n, t, bank="1"):
             if c >= CHUNKS:
                 return
             xc, xsc = xcs[c]
-            acc = ps_s1.tile([P, CW], F32, name="acc1")
+            if bank == "1":
+                acc = ps_s1.tile([P, CW], F32, name="acc1")
+            else:
+                acc = ps_s2.tile([P, BLK], F32, name="acc2")
             nc.tensor.matmul_mx(
                 out=acc[:],
                 lhsT=w1c[n][:, t * P : (t + 1) * P].bitcast(FP8X4),
@@ -298,7 +301,7 @@ def tile_blockdiagmnistconvertible_pa_t_kernel(tc, x, W1, b1, Wb, bb, out):
                 acc = ps_s1.tile([P, CW], F32, name="acc1")
                 nc.tensor.matmul(out=acc[:], lhsT=junk[:, :P], rhs=junk[:], start=True, stop=True)
 
-        warm(4)
+        warm(5)
         x_half(0, 0, "S")
         x_half(0, 1, "V")
         w1_half(0, 0, "V", "A")
@@ -307,17 +310,20 @@ def tile_blockdiagmnistconvertible_pa_t_kernel(tc, x, W1, b1, Wb, bb, out):
         quantise(w1g[0], w1c[0], w1sc[0])
         w1_half(1, 0, "V", "A")
         w1_half(1, 1, "S")
-        s1(0, 0, 0, "V")
+        for t in range(4):
+            s1_mm(0, 0, t, "1112"[t])
+        s1_act(0, 0, 0, "V")
         quantise(w1g[1], w1c[1], w1sc[1])
-        s1(0, 0, 1, "S")
-        s1(0, 0, 2, "V")
-        s1(0, 0, 3, "S")
-        for t in range(3):
-            s1(0, 1, t, "S")
+        s1_act(0, 0, 1, "S")
+        s1_act(0, 0, 2, "V")
+        s1_act(0, 0, 3, "S")
+        for t in range(4):
+            s1_mm(0, 1, t, "2211"[t])
+        for t in range(4):
+            s1_act(0, 1, t, "S")
         regroup(0, 0)
         x_half(1, 0, "V")
         h_quant(0, 0)
-        s1(0, 1, 3, "S")
         x_half(1, 1, "S")
         wb_half(0, 0, "S", "A")
         wb_half(0, 1, "S", "A")
@@ -339,6 +345,7 @@ def tile_blockdiagmnistconvertible_pa_t_kernel(tc, x, W1, b1, Wb, bb, out):
         s1_act(1, 0, 1)
         s1_act(1, 0, 2)
         s1_act(1, 0, 3)
+
 
         s2_add(0, 0)
         s2_mm(0, 3)
@@ -382,7 +389,6 @@ def tile_blockdiagmnistconvertible_pa_t_kernel(tc, x, W1, b1, Wb, bb, out):
         s1_mm(2, 0, 3)
         s1_act(2, 0, 2)
         finish(0, 2, "S")
-        x_tr(4)
         s1_mm(2, 1, 0)
         s1_mm(2, 1, 1)
         relu_part(0, 3, "V", 896, HID)
@@ -392,10 +398,14 @@ def tile_blockdiagmnistconvertible_pa_t_kernel(tc, x, W1, b1, Wb, bb, out):
 
         for c in range(1, CHUNKS):
             last = c == CHUNKS - 1
-            x_copy(c + 3)
+            if c > 1:
+                x_copy(c + 3)
             s1_act(c + 1, 1, 0)
             s2_add(c, 0)
             s2_mm(c, 3)
+            if c == 1:
+                x_tr(4)
+                x_copy(4)
             s2_add(c, 1)
             s2_mm(c, 4)
             s1_mm(c + 1, 1, 2)
@@ -429,7 +439,8 @@ def tile_blockdiagmnistconvertible_pa_t_kernel(tc, x, W1, b1, Wb, bb, out):
                 finish(c, 2, "S", 0, BLK)
                 finish(c, 2, "G", BLK, HID)
             else:
-                finish(c, 2, "S")
+                relu_part(c, 2, "G", 768, HID)
+                finish(c, 2, "S", 0, HID, 768)
             s1_mm(c + 2, 0, 2)
             s2_add(c, 6)
             if last:

from contextlib import ExitStack

import concourse.bass as bass
import concourse.mybir as mybir
import concourse.tile as tile
from concourse.masks import make_identity

F32 = mybir.dt.float32
BF16 = mybir.dt.bfloat16
U32 = mybir.dt.uint32
U8 = mybir.dt.uint8
FP8X4 = mybir.dt.float8_e4m3fn_x4
ALU = mybir.AluOpType
ACT = mybir.ActivationFunctionType

P = 128
B, IN, HID, BLK = 4096, 512, 1024, 512
NB = HID // BLK
ROWS_PER_PART = B // P
TILES = 4
CHUNKS = ROWS_PER_PART // TILES
CW = TILES * P
F32_MAX = 3.4028234663852886e38

FLOPS = 2 * B * HID * IN + 2 * B * HID * BLK


def tile_blockdiagmnistconvertible_pa_t_kernel(tc, x, W1, b1, Wb, bb, out):
    nc = tc.nc
    with ExitStack() as ctx:
        const = ctx.enter_context(tc.tile_pool(name="const", bufs=1))
        rows = ctx.enter_context(tc.tile_pool(name="rows", bufs=30))
        win = ctx.enter_context(tc.tile_pool(name="win", bufs=1))
        wq = ctx.enter_context(tc.tile_pool(name="wq", bufs=1))
        wgp = ctx.enter_context(tc.tile_pool(name="wgp", bufs=2))
        xq = ctx.enter_context(tc.tile_pool(name="xq", bufs=3))
        hp = ctx.enter_context(tc.tile_pool(name="hp", bufs=4))
        gp = ctx.enter_context(tc.tile_pool(name="gp", bufs=3))
        codes = ctx.enter_context(tc.tile_pool(name="codes", bufs=3))
        ps_tr = ctx.enter_context(tc.psum_pool(name="ps_tr", bufs=2))
        ps_s1 = ctx.enter_context(tc.psum_pool(name="ps_s1", bufs=3))
        ps_s2 = ctx.enter_context(tc.psum_pool(name="ps_s2", bufs=3))
        ctx.enter_context(tc.manual_schedule())

        x_v = x.rearrange("(p i) k -> p (i k)", i=ROWS_PER_PART)
        out_v = out.rearrange("(p i) o -> p (i o)", i=ROWS_PER_PART)

        xs = []
        for c in range(CHUNKS):
            row = rows.tile([P, TILES * IN], BF16, name="row")
            xs.append(row)
        w1s = [win.tile([P, 4 * IN], BF16, name="w1s%d" % n) for n in range(NB)]
        wbs = [win.tile([P, 4 * BLK], BF16, name="wbs%d" % n) for n in range(NB)]

        def load_x(c, parts=1):
            w = TILES * IN // parts
            for h in range(parts):
                lo = c * TILES * IN + h * w
                nc.sync.dma_start(out=xs[c][:, h * w : (h + 1) * w], in_=x_v[:, lo : lo + w])

        def load_w1(n, parts=1):
            src = W1[n * BLK : (n + 1) * BLK, :].rearrange("(p t) k -> p (t k)", t=4)
            w = 4 * IN // parts
            for h in range(parts):
                nc.sync.dma_start(
                    out=w1s[n][:, h * w : (h + 1) * w], in_=src[:, h * w : (h + 1) * w]
                )

        def load_wb(n):
            nc.sync.dma_start(
                out=wbs[n][:].rearrange("p (j k) -> p j k", j=4),
                in_=Wb[n].rearrange("(j p) k -> p j k", p=P),
            )

        b1b = const.tile([P, 2 * 4], BF16, name="b1b")
        b1f = const.tile([P, 2 * 4], F32, name="b1f")
        bbb = const.tile([P, HID], BF16, name="bbb")
        ident = const.tile([P, P], F32, name="ident")
        nc.scalar.dma_start(
            out=b1b[:].rearrange("p (n t) -> p n t", t=4),
            in_=b1.rearrange("(n p t) -> p n t", n=NB, t=4),
        )
        make_identity(nc, ident[:])
        load_x(0, 2)
        load_w1(0, 2)
        load_w1(1)
        load_x(1)
        load_wb(0)
        load_wb(1)
        nc.sync.dma_start(out=bbb[:], in_=bb.partition_broadcast(P))
        for c in range(2, CHUNKS):
            load_x(c)
        def copy_words(eng, dst, src):
            if eng == "S":
                nc.scalar.copy(out=dst, in_=src)
            else:
                nc.vector.tensor_copy(out=dst, in_=src)

        def transposes(src_words, h, bank="T"):
            if bank == "T":
                pt = ps_tr.tile([P, 512], F32, name="pt")
            else:
                pt = ps_s2.tile([P, BLK], F32, name="acc2")
            for il in range(2):
                for u in range(2):
                    nc.tensor.transpose(
                        pt[:, u * 256 + il * P : u * 256 + (il + 1) * P],
                        src_words(2 * h + il, u),
                        ident[:],
                    )
            return pt

        def interleave(pt, grouped, h, eng):
            g32 = grouped[:].bitcast(F32).rearrange("p (c u) -> p c u", u=2)
            copy_words(
                eng,
                g32[:, h * 256 : (h + 1) * 256, :],
                pt[:].rearrange("p (u c) -> p c u", u=2),
            )

        def transpose_half(src_words, grouped, h, eng, bank="T"):
            interleave(transposes(src_words, h, bank), grouped, h, eng)

        def quantise(grouped, words, scales):
            nc.vector.quantize_mx(out=words[:].bitcast(FP8X4), scales=scales[:], in_=grouped[:])

        w1c = [wq.tile([P, 512], U32, name="w1c%d" % n, align_bytes=64) for n in range(NB)]
        w1sc = [wq.tile([P, 512], U8, name="w1sc%d" % n, align_bytes=64) for n in range(NB)]
        wbc = [wq.tile([P, 512], U32, name="wbc%d" % n, align_bytes=64) for n in range(NB)]
        wbsc = [wq.tile([P, 512], U8, name="wbsc%d" % n, align_bytes=64) for n in range(NB)]
        w1g = [wq.tile([P, 2048], BF16, name="w1g%d" % n, align_bytes=64) for n in range(NB)]
        wbg = [wq.tile([P, 2048], BF16, name="wbg%d" % n, align_bytes=64) for n in range(NB)]
        xgs, xcs, hTs, hgs, hcs, zs, acc1s, acc2s, xps = {}, {}, {}, {}, {}, {}, {}, {}, {}

        def w1_half(n, h, eng, bank="T"):
            w32 = w1s[n][:].bitcast(F32).rearrange("p (t q u) -> p t q u", t=4, u=2)
            transpose_half(lambda t, u: w32[:, t, :, u], w1g[n], h, eng, bank)

        def wb_half(n, h, eng, bank="T"):
            w32 = wbs[n][:].bitcast(F32).rearrange("p (j q u) -> p j q u", j=4, u=2)
            transpose_half(lambda j, u: w32[:, j, :, u], wbg[n], h, eng, bank)

        def x_tr(c, halves=(0, 1)):
            if c >= CHUNKS:
                return
            x32 = xs[c][:].bitcast(F32).rearrange("p (i q u) -> p i q u", i=TILES, u=2)
            for h in halves:
                xps[(c, h)] = transposes(lambda i, u: x32[:, i, :, u], h)

        def x_copy(c, halves=(0, 1), eng="S"):
            if c >= CHUNKS:
                return
            if halves[0] == 0:
                xg = xq.tile([P, 2048], BF16, name="xg", align_bytes=64)
                xgs[c] = xg
            for h in halves:
                interleave(xps[(c, h)], xgs[c], h, eng)

        def x_half(c, h, eng="S"):
            x_tr(c, (h,))
            x_copy(c, (h,), eng)

        def x_quant(c):
            if c >= CHUNKS:
                return
            xc = codes.tile([P, CW], U32, name="xc", align_bytes=64)
            xsc = codes.tile([P, CW], U8, name="xsc", align_bytes=64)
            quantise(xgs[c], xc, xsc)
            xcs[c] = (xc, xsc)

        def s1_mm(c, n, t, bank="1"):
            if c >= CHUNKS:
                return
            xc, xsc = xcs[c]
            if bank == "1":
                acc = ps_s1.tile([P, CW], F32, name="acc1")
            else:
                acc = ps_s2.tile([P, BLK], F32, name="acc2")
            nc.tensor.matmul_mx(
                out=acc[:],
                lhsT=w1c[n][:, t * P : (t + 1) * P].bitcast(FP8X4),
                lhsT_scale=w1sc[n][:, t * P : (t + 1) * P],
                rhs=xc[:].bitcast(FP8X4),
                rhs_scale=xsc[:],
                start=True,
                stop=True,
            )
            acc1s[(c, n, t)] = acc

        def s1_act(c, n, t, eng="S"):
            if c >= CHUNKS:
                return
            if t == 0:
                hT = hp.tile([P, 4 * CW], BF16, name="hT")
                hTs[(c, n)] = hT
            acc = acc1s[(c, n, t)]
            hT = hTs[(c, n)]
            if paired(c, n):
                dst = hT[:].rearrange("p (u c e) -> p u e c", u=2, e=2)[:, t // 2, t % 2]
            else:
                dst = hT[:, t * CW : (t + 1) * CW]
            bias = b1f[:, 4 * n + t : 4 * n + t + 1]
            if eng == "S":
                nc.scalar.activation(out=dst, in_=acc[:], func=ACT.Relu, bias=bias, scale=1.0)
            else:
                nc.vector.tensor_scalar(
                    out=dst, in0=acc[:], scalar1=bias, scalar2=0.0, op0=ALU.add, op1=ALU.max
                )

        def s1(c, n, t, eng="S"):
            s1_mm(c, n, t)
            s1_act(c, n, t, eng)

        def paired(c, n):
            return c > 1 and n == 1 or c == CHUNKS - 1

        def regroup(c, n, eng="V"):
            if c >= CHUNKS:
                return
            hg = gp.tile([P, 4 * CW], BF16, name="hg", align_bytes=64)
            hgs[(c, n)] = hg
            if paired(c, n):
                copy_words(
                    eng,
                    hg[:].bitcast(F32).rearrange("p (c i u) -> p c u i", i=2, u=2),
                    hTs[(c, n)][:].bitcast(F32).rearrange("p (u c i) -> p c u i", u=2, i=2),
                )
                return
            dst = hgs[(c, n)][:].rearrange("p (c i t) -> p c t i", i=4, t=4)
            src = hTs[(c, n)][:].rearrange("p (t c i) -> p c t i", t=4, i=4)
            copy_words(eng, dst, src)

        def h_quant(c, n):
            if c >= CHUNKS:
                return
            hc = codes.tile([P, CW], U32, name="hc%d" % n, align_bytes=64)
            hsc = codes.tile([P, CW], U8, name="hsc%d" % n, align_bytes=64)
            quantise(hgs[(c, n)], hc, hsc)
            hcs[(c, n)] = (hc, hsc)

        def relu2(eng, ap):
            if eng == "V":
                nc.vector.tensor_scalar_max(out=ap, in0=ap, scalar1=0.0)
            elif eng == "S":
                nc.scalar.activation(out=ap, in_=ap, func=ACT.Relu)
            else:
                nc.gpsimd.tensor_scalar(
                    out=ap, in0=ap, scalar1=F32_MAX, scalar2=0.0, op0=ALU.min, op1=ALU.max
                )

        def s2_mm(c, k):
            if c >= CHUNKS:
                return
            il, n = divmod(k, NB)
            hc, hsc = hcs[(c, n)]
            acc = ps_s2.tile([P, BLK], F32, name="acc2")
            nc.tensor.matmul_mx(
                out=acc[:],
                lhsT=hc[:, il * P : (il + 1) * P].bitcast(FP8X4),
                lhsT_scale=hsc[:, il * P : (il + 1) * P],
                rhs=wbc[n][:].bitcast(FP8X4),
                rhs_scale=wbsc[n][:],
                start=True,
                stop=True,
            )
            acc2s[(c, k)] = acc

        def s2_add(c, k):
            il, n = divmod(k, NB)
            if n == 0:
                row = rows.tile([P, HID], F32, name="row")
                zs[(c, il)] = row
            z = zs[(c, il)]
            acc = acc2s[(c, k)]
            nc.vector.tensor_tensor(
                out=z[:, n * BLK : (n + 1) * BLK],
                in0=acc[:],
                in1=bbb[:, n * BLK : (n + 1) * BLK],
                op=ALU.add,
            )

        def relu_part(c, il, eng, lo, hi):
            relu2(eng, zs[(c, il)][:, lo:hi])

        def finish(c, il, eng, lo=0, hi=HID, relu_hi=None):
            relu2(eng, zs[(c, il)][:, lo : relu_hi or hi])
            base = (c * TILES + il) * HID
            nc.sync.dma_start(out=out_v[:, base + lo : base + hi], in_=zs[(c, il)][:, lo:hi])

        junk = const.tile([P, BLK], BF16, name="junk")
        nc.vector.memset(junk[:], 0.0)
        nc.vector.tensor_copy(out=b1f[:], in_=b1b[:])

        def warm_tr(count):
            for i in range(count):
                pt = ps_tr.tile([P, 512], F32, name="pt")
                nc.tensor.matmul(out=pt[:], lhsT=junk[:, :P], rhs=junk[:], start=True, stop=True)

        def warm(count):
            for i in range(count):
                acc = ps_s1.tile([P, CW], F32, name="acc1")
                nc.tensor.matmul(out=acc[:], lhsT=junk[:, :P], rhs=junk[:], start=True, stop=True)

        warm(5)
        x_half(0, 0, "S")
        x_half(0, 1, "V")
        w1_half(0, 0, "V", "A")
        w1_half(0, 1, "S", "A")
        x_quant(0)
        quantise(w1g[0], w1c[0], w1sc[0])
        w1_half(1, 0, "V", "A")
        w1_half(1, 1, "S")
        for t in range(4):
            s1_mm(0, 0, t, "1112"[t])
        s1_act(0, 0, 0, "V")
        quantise(w1g[1], w1c[1], w1sc[1])
        s1_act(0, 0, 1, "S")
        s1_act(0, 0, 2, "V")
        s1_act(0, 0, 3, "S")
        for t in range(4):
            s1_mm(0, 1, t, "2211"[t])
        for t in range(4):
            s1_act(0, 1, t, "S")
        regroup(0, 0)
        x_half(1, 0, "V")
        h_quant(0, 0)
        x_half(1, 1, "S")
        wb_half(0, 0, "S", "A")
        wb_half(0, 1, "S", "A")
        regroup(0, 1)
        x_quant(1)
        wb_half(1, 0, "S", "A")
        wb_half(1, 1, "S", "A")
        quantise(wbg[0], wbc[0], wbsc[0])
        h_quant(0, 1)
        quantise(wbg[1], wbc[1], wbsc[1])
        s1_mm(1, 0, 0)
        s2_mm(0, 0)
        s1_mm(1, 0, 1)
        s2_mm(0, 1)
        s1_mm(1, 0, 2)
        s1_act(1, 0, 0)
        s2_mm(0, 2)
        s1_mm(1, 0, 3)
        s1_act(1, 0, 1)
        s1_act(1, 0, 2)
        s1_act(1, 0, 3)


        s2_add(0, 0)
        s2_mm(0, 3)
        s1_mm(1, 1, 0)
        s2_add(0, 1)
        s2_mm(0, 4)
        s1_mm(1, 1, 1)
        s1_mm(1, 1, 2)
        s1_act(1, 1, 0)
        finish(0, 0, "G")
        s2_add(0, 2)
        s2_mm(0, 5)
        s1_act(1, 1, 1)
        s2_add(0, 3)
        s2_mm(0, 6)
        finish(0, 1, "G")
        s1_act(1, 1, 2)
        s2_add(0, 4)
        s2_mm(0, 7)
        s1_mm(1, 1, 3)
        x_tr(2)
        s1_act(1, 1, 3)
        s2_add(0, 5)
        x_copy(2)
        x_tr(3)
        s2_add(0, 6)
        s2_add(0, 7)
        regroup(1, 0)
        x_quant(2)
        regroup(1, 1)
        for t in range(3):
            s1_mm(2, 0, t)
        x_copy(3)
        h_quant(1, 0)
        s1_act(2, 0, 0)
        s2_mm(1, 0)
        h_quant(1, 1)
        s1_act(2, 0, 1)
        s2_mm(1, 1)
        s2_mm(1, 2)
        s1_mm(2, 0, 3)
        s1_act(2, 0, 2)
        finish(0, 2, "S")
        s1_mm(2, 1, 0)
        s1_mm(2, 1, 1)
        relu_part(0, 3, "V", 896, HID)
        finish(0, 3, "G", 0, HID, 900)
        x_quant(3)
        s1_act(2, 0, 3)

        for c in range(1, CHUNKS):
            last = c == CHUNKS - 1
            if c > 1:
                x_copy(c + 3)
            s1_act(c + 1, 1, 0)
            s2_add(c, 0)
            s2_mm(c, 3)
            if c == 1:
                x_tr(4)
                x_copy(4)
            s2_add(c, 1)
            s2_mm(c, 4)
            s1_mm(c + 1, 1, 2)
            if last:
                finish(c, 0, "S", 0, BLK)
                finish(c, 0, "G", BLK, HID)
            else:
                finish(c, 0, "G")
            s2_add(c, 2)
            s2_mm(c, 5)
            s1_act(c + 1, 1, 1)
            s2_add(c, 3)
            s2_mm(c, 6)
            s1_mm(c + 1, 1, 3)
            if last:
                finish(c, 1, "S", 0, BLK)
                finish(c, 1, "G", BLK, HID)
            else:
                finish(c, 1, "G")
            s1_act(c + 1, 1, 2)
            s2_add(c, 4)
            s2_mm(c, 7)
            s1_mm(c + 2, 0, 0)
            if c + 4 >= CHUNKS:
                warm_tr(2)
            x_tr(c + 4)
            s1_mm(c + 2, 0, 1)
            s1_act(c + 1, 1, 3)
            s2_add(c, 5)
            if last:
                finish(c, 2, "S", 0, BLK)
                finish(c, 2, "G", BLK, HID)
            else:
                relu_part(c, 2, "G", 768, HID)
                finish(c, 2, "S", 0, HID, 768)
            s1_mm(c + 2, 0, 2)
            s2_add(c, 6)
            if last:
                finish(c, 3, "S", 0, BLK)
            s2_add(c, 7)
            regroup(c + 1, 0)
            regroup(c + 1, 1)
            h_quant(c + 1, 0)
            s1_act(c + 2, 0, 0)
            s1_mm(c + 2, 0, 3)
            s2_mm(c + 1, 0)
            h_quant(c + 1, 1)
            s1_act(c + 2, 0, 1)
            s2_mm(c + 1, 1)
            s2_mm(c + 1, 2)
            s1_act(c + 2, 0, 2)
            s1_mm(c + 2, 1, 0)
            s1_mm(c + 2, 1, 1)
            if last:
                finish(c, 3, "V", BLK, HID)
            else:
                relu_part(c, 3, "V", 896, HID)
                if c == CHUNKS - 2:
                    finish(c, 3, "S", 0, BLK)
                    finish(c, 3, "G", BLK, HID, 900)
                else:
                    finish(c, 3, "G", 0, HID, 900)
            x_quant(c + 3)
            s1_act(c + 2, 0, 3)
